import numpy as np
import ml_dtypes


def mxq(x, axis, fmt="e4m3"):
    dtype, down = {"e4m3": (ml_dtypes.float8_e4m3fn, 7), "e5m2": (ml_dtypes.float8_e5m2, 14)}[fmt]
    v = np.moveaxis(np.asarray(x, np.float32).astype(ml_dtypes.bfloat16).astype(np.float64), axis, -1)
    blocks = v.reshape(v.shape[:-1] + (-1, 32))
    amax = np.abs(blocks).max(-1, keepdims=True)
    byte = np.maximum(np.where(amax > 0, np.frexp(amax)[1] - 1 + 127, 0) - down, 1)
    scale = np.exp2(byte - 127.0)
    codes = (blocks / scale).astype(np.float32).astype(dtype).astype(np.float64)
    return np.moveaxis((codes * scale).reshape(v.shape), -1, axis)


WIDE = False


def mx_kscale(k):
    if not WIDE:
        return np.ones(k)
    levels = np.array([10, -10, 5, -5, 0])
    if k % 512:
        return np.exp2(np.random.permutation(np.resize(levels, k // 32))).repeat(32)
    a = np.empty((k // 512, 16))
    for p in range(k // 512):
        a[p, :8] = np.random.permutation(np.resize(levels, 8))
        for g in range(8):
            far = levels[np.abs(levels - a[p, g]) >= 10]
            a[p, g + 8] = far[np.random.randint(len(far))]
    return np.exp2(a.ravel()).repeat(32)


BF16 = ml_dtypes.bfloat16


def bf(x):
    return np.asarray(x, np.float32).astype(BF16)


def f64(x):
    return np.asarray(x).astype(np.float64)


L, B, D, F, TC = 8, 4096, 512, 1024, 4
EPS = 1e-5
NT = 100
ERF_C = 1.0 / np.cumprod(2.0 * np.arange(NT) + 1.0)


def erf(v):
    a = np.minimum(np.abs(v), 6.0)
    q = 2.0 * a * a
    acc = np.full_like(q, ERF_C[-1])
    for c in ERF_C[-2::-1]:
        acc = acc * q + c
    return np.sign(v) * (2.0 / np.sqrt(np.pi)) * a * np.exp(-a * a) * acc


def gelu(v):
    return 0.5 * v * (1.0 + erf(v / np.sqrt(2.0)))


def layer_norm(x, g, b):
    m = x.mean(-1, keepdims=True)
    v = ((x - m) ** 2).mean(-1, keepdims=True)
    return (x - m) / np.sqrt(v + EPS) * g + b


def setup_inputs():
    s, t = mx_kscale(D), mx_kscale(F)
    return {"z": bf(np.random.standard_normal((B, D)) * s),
            "W1": bf(np.random.standard_normal((D, F)) / np.sqrt(D) / s[:, None]),
            "b1": bf(np.random.standard_normal(F) * 0.3),
            "g1": bf((1.0 + 0.1 * np.random.standard_normal(F)) * t),
            "be1": bf(0.1 * np.random.standard_normal(F) * t),
            "W2": bf(np.random.standard_normal((F, D)) / np.sqrt(F) / t[:, None]),
            "b2": bf(np.random.standard_normal(D) * 0.3),
            "g2": bf(1.0 + 0.1 * np.random.standard_normal(D)),
            "be2": bf(0.1 * np.random.standard_normal(D))}


def reference(z, W1, b1, g1, be1, W2, b2, g2, be2):
    h = gelu(f64(bf(mxq(f64(z), 1, "e4m3") @ mxq(f64(W1), 0, "e4m3"))) + f64(b1))
    h = layer_norm(h, f64(g1), f64(be1))
    return layer_norm((mxq(h, 1, "e4m3") @ mxq(f64(W2), 0, "e4m3")) + f64(b2), f64(g2), f64(be2))

@@ -1,0 +1,484 @@
+from contextlib import ExitStack
+
+import concourse.mybir as mybir
+from concourse.masks import make_identity
+
+B, D, F = 4096, 512, 1024
+EPS = 1e-5
+FLOPS = 2 * B * D * F * 2
+
+F32 = mybir.dt.float32
+BF16 = mybir.dt.bfloat16
+U32 = mybir.dt.uint32
+U8 = mybir.dt.uint8
+FP8X4 = mybir.dt.float8_e4m3fn_x4
+ALU = mybir.AluOpType
+ACT = mybir.ActivationFunctionType
+
+P = 128
+NT = B // P
+GT = 4
+NG = NT // GT
+ON_SCALAR = [3]
+BANK_DT = BF16
+
+
+def tile_emaaggregator_pa_t_kernel(tc, z, W1, b1, g1, be1, W2, b2, g2, be2, out):
+    nc = tc.nc
+    z_view = z.rearrange("(p i) k -> p i k", i=NT)
+    out_view = out.rearrange("(p i) d -> p i d", i=NT)
+
+    with ExitStack() as ctx:
+        const = ctx.enter_context(tc.tile_pool(name="const", bufs=1))
+        work = ctx.enter_context(tc.tile_pool(name="work", bufs=2))
+        stats = ctx.enter_context(tc.tile_pool(name="stats", bufs=3))
+        psum = ctx.enter_context(tc.psum_pool(name="psum", bufs=2))
+        ctx.enter_context(tc.manual_schedule())
+
+        live = {}
+
+        def ok(grp):
+            return 0 <= grp < NG
+
+        b1n = const.tile([P, F], BF16, name="b1n")
+        nc.scalar.dma_start(out=b1n[:], in_=b1.partition_broadcast(P))
+
+        zs = []
+        w1raw = []
+        w2raw = []
+
+        def load_z(grp):
+            t = const.tile([P, GT, D], BF16, name="zs%d" % grp)
+            nc.sync.dma_start(out=t[:], in_=z_view[:, GT * grp : GT * (grp + 1), :])
+            zs.append(t)
+
+        load_z(0)
+        w1_view = W1.rearrange("(p j) c -> p j c", j=4)
+        for g in range(2):
+            t = const.tile([P, 4, 512], BF16, name="w1raw%d" % g)
+            nc.sync.dma_start(out=t[:], in_=w1_view[:, :, 512 * g : 512 * (g + 1)])
+            w1raw.append(t)
+        load_z(1)
+        for g in range(2):
+            t = const.tile([P, 4, 512], BF16, name="w2raw%d" % g)
+            nc.sync.dma_start(out=t[:], in_=W2[512 * g : 512 * (g + 1), :].rearrange("(p j) d -> p j d", j=4))
+            w2raw.append(t)
+        for grp in range(2, NG):
+            load_z(grp)
+        g1b = const.tile([P, 2, 4], BF16, name="g1b")
+        nc.sync.dma_start(out=g1b[:], in_=g1.rearrange("(g p t) -> p g t", g=2, t=4))
+        be1b = const.tile([P, 2, 4], BF16, name="be1b")
+        nc.sync.dma_start(out=be1b[:], in_=be1.rearrange("(g p t) -> p g t", g=2, t=4))
+        b2bc = const.tile([P, D], BF16, name="b2bc")
+        nc.sync.dma_start(out=b2bc[:], in_=b2.partition_broadcast(P))
+        g2bc = const.tile([P, D], BF16, name="g2bc")
+        nc.sync.dma_start(out=g2bc[:], in_=g2.partition_broadcast(P))
+        be2bc = const.tile([P, D], BF16, name="be2bc")
+        nc.sync.dma_start(out=be2bc[:], in_=be2.partition_broadcast(P))
+
+        neg_half = const.tile([P, GT], F32, name="neg_half")
+        nc.gpsimd.memset(neg_half[:], -0.5)
+        warm = const.tile([P, 1], F32, name="warm")
+        nc.scalar.activation(out=warm[:], in_=neg_half[:, 0:1], func=ACT.Gelu)
+        ident = const.tile([P, P], F32, name="ident")
+        make_identity(nc, ident[:])
+
+        def z_transpose(grp, h):
+            if not ok(grp):
+                return
+            zt = psum.tile([P, 2, 2, P], F32, name="zt", tag="bank", bufs=8)
+            for jj in range(2):
+                words = zs[grp][:, 2 * h + jj, :].bitcast(F32)
+                for u in range(2):
+                    nc.tensor.transpose(zt[:, jj, u, :], words[:, u:256:2], ident[:])
+            live["zt", grp, h] = zt
+
+        def z_copy(grp, h):
+            if not ok(grp):
+                return
+            if h == 0:
+                live["zg", grp] = work.tile([P, GT * P * 4], BF16, name="zg", tag="zg", bufs=2, align_bytes=64)
+            zgw = live["zg", grp][:].bitcast(F32).rearrange("p (j r u) -> p j r u", j=GT, u=2)
+            nc.scalar.copy(
+                out=zgw[:, 2 * h : 2 * h + 2, :, :], in_=live["zt", grp, h][:].rearrange("p j u r -> p j r u")
+            )
+
+        def z_quantise(grp):
+            if not ok(grp):
+                return
+            zc = work.tile([P, GT * P], U32, name="zc", tag="zc", bufs=2, align_bytes=64)
+            zsc = work.tile([P, GT * P], U8, name="zsc", tag="zsc", bufs=2, align_bytes=64)
+            nc.vector.quantize_mx(out=zc[:].bitcast(FP8X4), scales=zsc[:], in_=live["zg", grp][:])
+            live["zq", grp] = (zc, zsc)
+
+        def matmul_1(grp, i):
+            if not ok(grp):
+                return
+            zc, zsc = live["zq", grp]
+            cols = slice(P * i, P * (i + 1))
+            for g in range(2):
+                u = psum.tile([P, 512], BANK_DT, name="u", tag="bank", bufs=8)
+                nc.tensor.matmul_mx(
+                    out=u[:],
+                    lhsT=zc[:, cols].bitcast(FP8X4),
+                    lhsT_scale=zsc[:, cols],
+                    rhs=w1c[g][:].bitcast(FP8X4),
+                    rhs_scale=w1s[g][:],
+                    start=True,
+                    stop=True,
+                )
+                live["u", grp, i, g] = u
+
+        def add_b1(grp, i):
+            if not ok(grp):
+                return
+            x = work.tile([P, F], F32, name="x", tag="x", bufs=2)
+            for g in range(2):
+                half = slice(512 * g, 512 * (g + 1))
+                nc.vector.tensor_tensor(out=x[:, half], in0=live["u", grp, i, g][:], in1=b1p[:, half], op=ALU.add)
+            live["x", grp, i] = x
+
+        def gelu(grp, i):
+            if not ok(grp):
+                return
+            if i == 0:
+                live["sa", grp] = stats.tile([P, GT], F32, name="sa", tag="sa")
+            a = work.tile([P, F], F32, name="a", tag="a", bufs=6)
+            nc.scalar.activation(
+                out=a[:], in_=live["x", grp, i][:], func=ACT.Gelu, accum_out=live["sa", grp][:, i : i + 1]
+            )
+            live["a", grp, i] = a
+
+        def square_1(grp, i):
+            if not ok(grp):
+                return
+            if i == 0:
+                live["sq", grp] = stats.tile([P, GT], F32, name="sq", tag="sq")
+            junk = work.tile([P, F], BF16, name="junk", tag="junk", bufs=1)
+            nc.scalar.activation(
+                out=junk[:],
+                in_=live["a", grp, i][:],
+                func=ACT.Square,
+                scale=-float(F),
+                bias=live["sa", grp][:, i : i + 1],
+                accum_out=live["sq", grp][:, i : i + 1],
+            )
+
+        def neg_mean_1(grp):
+            if not ok(grp):
+                return
+            nm = stats.tile([P, GT], F32, name="nm", tag="nm")
+            nc.vector.tensor_scalar(out=nm[:], in0=live["sa", grp][:], scalar1=-1.0 / F, scalar2=None, op0=ALU.mult)
+            live["nm", grp] = nm
+
+        def var_eps_1(grp):
+            if not ok(grp):
+                return
+            ve = stats.tile([P, GT], F32, name="ve", tag="ve")
+            nc.vector.tensor_scalar(
+                out=ve[:], in0=live["sq", grp][:], scalar1=1.0 / F**3, scalar2=EPS, op0=ALU.mult, op1=ALU.add
+            )
+            live["ve", grp] = ve
+
+        def rstd_1(grp):
+            if not ok(grp):
+                return
+            rs = stats.tile([P, GT], F32, name="rs", tag="rs")
+            nc.gpsimd.tensor_tensor(out=rs[:], in0=live["ve", grp][:], in1=neg_half[:], op=ALU.pow)
+            nr = stats.tile([P, GT], F32, name="nr", tag="nr")
+            nc.gpsimd.tensor_tensor(out=nr[:], in0=live["nm", grp][:], in1=rs[:], op=ALU.mult)
+            live["rs", grp] = rs
+            live["nr", grp] = nr
+
+        def normalise(grp, i):
+            if not ok(grp):
+                return
+            col = slice(i, i + 1)
+            xh = work.tile([P, F], F32, name="xh", tag="xh", bufs=4)
+            if i in ON_SCALAR:
+                nc.scalar.activation(
+                    out=xh[:],
+                    in_=live["a", grp, i][:],
+                    func=ACT.Identity,
+                    scale=live["rs", grp][:, col],
+                    bias=live["nr", grp][:, col],
+                )
+            else:
+                nc.vector.tensor_scalar(
+                    out=xh[:],
+                    in0=live["a", grp, i][:],
+                    scalar1=live["nm", grp][:, col],
+                    scalar2=live["rs", grp][:, col],
+                    op0=ALU.add,
+                    op1=ALU.mult,
+                )
+            live["xh", grp, i] = xh
+
+        def h_transpose(grp, blk):
+            if not ok(grp):
+                return
+            ht = psum.tile([P, GT * P], F32, name="ht", tag="bank", bufs=8)
+            for i in range(GT):
+                nc.tensor.transpose(ht[:, P * i : P * (i + 1)], live["xh", grp, i][:, P * blk : P * (blk + 1)], ident[:])
+            live["ht", grp, blk] = ht
+
+        def affine_1(grp, blk):
+            if not ok(grp):
+                return
+            if blk == 0:
+                live["hT", grp] = work.tile([P, 8, GT * P], BF16, name="hT", tag="hT", bufs=2)
+            nc.scalar.activation(
+                out=live["hT", grp][:, blk, :],
+                in_=live["ht", grp, blk][:],
+                func=ACT.Identity,
+                scale=g1c[:, blk : blk + 1],
+                bias=be1c[:, blk : blk + 1],
+            )
+
+        def interleave(grp, g):
+            if not ok(grp):
+                return
+            hg = work.tile([P, GT * P, 4], BF16, name="hg", tag="hg", bufs=2, align_bytes=64)
+            nc.vector.tensor_copy(
+                out=hg[:].rearrange("p (c i) t -> p c t i", i=4),
+                in_=live["hT", grp][:, 4 * g : 4 * g + 4, :].rearrange("p t (c i) -> p c t i", i=4),
+            )
+            live["hg", grp, g] = hg
+
+        def h_quantise(grp, g):
+            if not ok(grp):
+                return
+            hc = work.tile([P, GT * P], U32, name="hc", tag="hc", bufs=4, align_bytes=64)
+            hs = work.tile([P, GT * P], U8, name="hs", tag="hs", bufs=4, align_bytes=64)
+            nc.vector.quantize_mx(
+                out=hc[:].bitcast(FP8X4), scales=hs[:], in_=live["hg", grp, g][:].rearrange("p n t -> p (n t)")
+            )
+            live["hq", grp, g] = (hc, hs)
+
+        def matmul_2(grp, i):
+            if not ok(grp):
+                return
+            cols = slice(P * i, P * (i + 1))
+            o = psum.tile([P, D], F32, name="o", tag="bank", bufs=8)
+            for g in range(2):
+                hc, hs = live["hq", grp, g]
+                nc.tensor.matmul_mx(
+                    out=o[:],
+                    lhsT=hc[:, cols].bitcast(FP8X4),
+                    lhsT_scale=hs[:, cols],
+                    rhs=w2c[g][:].bitcast(FP8X4),
+                    rhs_scale=w2s[g][:],
+                    start=(g == 0),
+                    stop=(g == 1),
+                )
+            live["o", grp, i] = o
+
+        def add_b2(grp, i):
+            if not ok(grp):
+                return
+            if i == 0:
+                live["sy", grp] = stats.tile([P, GT], F32, name="sy", tag="sy")
+            y = work.tile([P, D], F32, name="y", tag="y", bufs=4)
+            nc.vector.scalar_tensor_tensor(
+                out=y[:],
+                in0=live["o", grp, i][:],
+                scalar=1.0,
+                in1=b2bc[:],
+                op0=ALU.mult,
+                op1=ALU.add,
+                accum_out=live["sy", grp][:, i : i + 1],
+            )
+            live["y", grp, i] = y
+
+        def square_2(grp, i):
+            if not ok(grp):
+                return
+            if i == 0:
+                live["sq2", grp] = stats.tile([P, GT], F32, name="sq2", tag="sq2")
+            junk2 = work.tile([P, D], BF16, name="junk2", tag="junk2", bufs=1)
+            nc.scalar.activation(
+                out=junk2[:],
+                in_=live["y", grp, i][:],
+                func=ACT.Square,
+                scale=-float(D),
+                bias=live["sy", grp][:, i : i + 1],
+                accum_out=live["sq2", grp][:, i : i + 1],
+            )
+
+        def neg_mean_2(grp):
+            if not ok(grp):
+                return
+            nm2 = stats.tile([P, GT], F32, name="nm2", tag="nm2")
+            nc.vector.tensor_scalar(out=nm2[:], in0=live["sy", grp][:], scalar1=-1.0 / D, scalar2=None, op0=ALU.mult)
+            live["nm2", grp] = nm2
+
+        def var_eps_2(grp):
+            if not ok(grp):
+                return
+            ve2 = stats.tile([P, GT], F32, name="ve2", tag="ve2")
+            nc.vector.tensor_scalar(
+                out=ve2[:], in0=live["sq2", grp][:], scalar1=1.0 / D**3, scalar2=EPS, op0=ALU.mult, op1=ALU.add
+            )
+            live["ve2", grp] = ve2
+
+        def rstd_2(grp):
+            if not ok(grp):
+                return
+            rs2 = stats.tile([P, GT], F32, name="rs2", tag="rs2")
+            nc.gpsimd.tensor_tensor(out=rs2[:], in0=live["ve2", grp][:], in1=neg_half[:], op=ALU.pow)
+            live["rs2", grp] = rs2
+
+        def centre_gain(grp, i):
+            if not ok(grp):
+                return
+            q = work.tile([P, D], F32, name="q", tag="q", bufs=4)
+            nc.vector.scalar_tensor_tensor(
+                out=q[:],
+                in0=live["y", grp, i][:],
+                scalar=live["nm2", grp][:, i : i + 1],
+                in1=g2bc[:],
+                op0=ALU.add,
+                op1=ALU.mult,
+            )
+            live["q", grp, i] = q
+
+        def scale_shift(grp, i):
+            if not ok(grp):
+                return
+            ot = work.tile([P, D], F32, name="ot", tag="ot", bufs=4)
+            nc.vector.scalar_tensor_tensor(
+                out=ot[:],
+                in0=live["q", grp, i][:],
+                scalar=live["rs2", grp][:, i : i + 1],
+                in1=be2bc[:],
+                op0=ALU.mult,
+                op1=ALU.add,
+            )
+            live["ot", grp, i] = ot
+
+        def store(grp, i):
+            if not ok(grp):
+                return
+            nc.sync.dma_start(out=out_view[:, GT * grp + i, :], in_=live["ot", grp, i][:])
+
+        z_transpose(0, 0)
+        w1g = []
+        for g in range(2):
+            w1g.append(const.tile([P, 2048], BF16, name="w1g%d" % g, align_bytes=64))
+        dst = [w1g[g][:].rearrange("p (t m j) -> p t m j", t=4, j=4) for g in range(2)]
+        src = [w1raw[g][:].rearrange("p j (m t) -> p t m j", t=4) for g in range(2)]
+        w1c, w1s, w2c, w2s = [], [], [], []
+        for g in range(2):
+            w1c.append(const.tile([P, 512], U32, name="w1c%d" % g, align_bytes=64))
+            w1s.append(const.tile([P, 512], U8, name="w1s%d" % g, align_bytes=64))
+        nc.vector.tensor_copy(out=dst[0][:, 0:2], in_=src[0][:, 0:2])
+        nc.vector.tensor_copy(out=dst[0][:, 2:4], in_=src[0][:, 2:4])
+        nc.scalar.copy(out=dst[1][:, 2:4], in_=src[1][:, 2:4])
+        z_copy(0, 0)
+        z_transpose(0, 1)
+        z_copy(0, 1)
+        nc.vector.tensor_copy(out=dst[1][:, 0:2], in_=src[1][:, 0:2])
+        nc.vector.quantize_mx(out=w1c[0][:].bitcast(FP8X4), scales=w1s[0][:], in_=w1g[0][:])
+        z_quantise(0)
+        nc.vector.quantize_mx(out=w1c[1][:].bitcast(FP8X4), scales=w1s[1][:], in_=w1g[1][:])
+        b1p = const.tile([P, F], BF16, name="b1p")
+        nc.scalar.copy(
+            out=b1p[:].rearrange("p (g t m) -> p g t m", g=2, t=4),
+            in_=b1n[:].rearrange("p (g m t) -> p g t m", g=2, t=4),
+        )
+        g1c = const.tile([P, 8], F32, name="g1c")
+        nc.gpsimd.tensor_copy(out=g1c[:], in_=g1b[:].rearrange("p g t -> p (g t)"))
+        be1c = const.tile([P, 8], F32, name="be1c")
+        nc.gpsimd.tensor_copy(out=be1c[:], in_=be1b[:].rearrange("p g t -> p (g t)"))
+
+        def prep_w2():
+            w2g = []
+            for g in range(2):
+                w2g.append(const.tile([P, 512, 4], BF16, name="w2g%d" % g, align_bytes=64))
+                nc.vector.tensor_copy(out=w2g[g][:], in_=w2raw[g][:].rearrange("p j d -> p d j"))
+            for g in range(2):
+                w2c.append(const.tile([P, 512], U32, name="w2c%d" % g, align_bytes=64))
+                w2s.append(const.tile([P, 512], U8, name="w2s%d" % g, align_bytes=64))
+                nc.vector.quantize_mx(
+                    out=w2c[g][:].bitcast(FP8X4), scales=w2s[g][:], in_=w2g[g][:].rearrange("p d j -> p (d j)")
+                )
+
+        for step in range(NG + 2):
+            if True:
+                z_transpose(step + 1, 0)
+                matmul_1(step, 0)
+                matmul_1(step, 1)
+                z_transpose(step + 1, 1)
+                matmul_1(step, 2)
+                var_eps_1(step - 1)
+                neg_mean_1(step - 1)
+                add_b1(step, 0)
+                rstd_1(step - 1)
+                normalise(step - 1, 0)
+                normalise(step - 1, 1)
+                z_copy(step + 1, 0)
+                normalise(step - 1, 2)
+                normalise(step - 1, 3)
+                h_transpose(step - 1, 0)
+                centre_gain(step - 2, 0)
+                gelu(step, 0)
+                var_eps_2(step - 2)
+                centre_gain(step - 2, 1)
+                h_transpose(step - 1, 1)
+                rstd_2(step - 2)
+                add_b1(step, 1)
+                h_transpose(step - 1, 2)
+                z_copy(step + 1, 1)
+                h_transpose(step - 1, 3)
+                affine_1(step - 1, 0)
+                add_b1(step, 2)
+                h_transpose(step - 1, 4)
+                affine_1(step - 1, 1)
+                h_transpose(step - 1, 5)
+                h_transpose(step - 1, 6)
+                affine_1(step - 1, 2)
+                z_quantise(step + 1)
+                h_transpose(step - 1, 7)
+                affine_1(step - 1, 3)
+                centre_gain(step - 2, 2)
+                matmul_1(step, 3)
+                affine_1(step - 1, 4)
+                interleave(step - 1, 0)
+                affine_1(step - 1, 5)
+                affine_1(step - 1, 6)
+                centre_gain(step - 2, 3)
+                affine_1(step - 1, 7)
+                h_quantise(step - 1, 0)
+                gelu(step, 1)
+                interleave(step - 1, 1)
+                square_1(step, 0)
+                h_quantise(step - 1, 1)
+                matmul_2(step - 1, 0)
+                square_1(step, 1)
+                add_b1(step, 3)
+                matmul_2(step - 1, 1)
+                gelu(step, 2)
+                scale_shift(step - 2, 0)
+                matmul_2(step - 1, 2)
+                scale_shift(step - 2, 1)
+                store(step - 2, 0)
+                matmul_2(step - 1, 3)
+                square_1(step, 2)
+                scale_shift(step - 2, 2)
+                store(step - 2, 1)
+                add_b2(step - 1, 0)
+                store(step - 2, 2)
+                gelu(step, 3)
+                add_b2(step - 1, 1)
+                add_b2(step - 1, 2)
+                square_1(step, 3)
+                add_b2(step - 1, 3)
+                scale_shift(step - 2, 3)
+                square_2(step - 1, 0)
+                neg_mean_2(step - 1)
+                square_2(step - 1, 1)
+                store(step - 2, 3)
+                square_2(step - 1, 2)
+                square_2(step - 1, 3)
+            if step == 0:
+                prep_w2()

@@ -19,8 +19,9 @@ P = 128
 NT = B // P
 GT = 4
 NG = NT // GT
-ON_SCALAR = [3]
-BANK_DT = BF16
+NPAIR = NT // 2
+BATCHES = [(0, 8), (8, 8), (16, 8), (24, 4), (28, 4)]
+ON_GPSIMD = 28
 
 
 def tile_emaaggregator_pa_t_kernel(tc, z, W1, b1, g1, be1, W2, b2, g2, be2, out):
@@ -40,35 +41,43 @@ def tile_emaaggregator_pa_t_kernel(tc, z, W1, b1, g1, be1, W2, b2, g2, be2, out)
         def ok(grp):
             return 0 <= grp < NG
 
-        b1n = const.tile([P, F], BF16, name="b1n")
+        def tile_ok(i):
+            return 0 <= i < NT
+
+        batch_of = {}
+        for first, count in BATCHES:
+            for j in range(count):
+                batch_of[first + j] = (first, j, count)
+
+        b1n = work.tile([P, F], BF16, name="b1n", tag="x", bufs=4)
         nc.scalar.dma_start(out=b1n[:], in_=b1.partition_broadcast(P))
 
-        zs = []
-        w1raw = []
-        w2raw = []
+        zs = {}
 
         def load_z(grp):
-            t = const.tile([P, GT, D], BF16, name="zs%d" % grp)
+            t = work.tile([P, GT, D], BF16, name="zs", tag="zs", bufs=4)
             nc.sync.dma_start(out=t[:], in_=z_view[:, GT * grp : GT * (grp + 1), :])
-            zs.append(t)
+            zs[grp] = t
 
+        w1raw = []
+        w2raw = []
         load_z(0)
         w1_view = W1.rearrange("(p j) c -> p j c", j=4)
         for g in range(2):
-            t = const.tile([P, 4, 512], BF16, name="w1raw%d" % g)
+            t = work.tile([P, 4, 512], BF16, name="w1raw", tag="wr", bufs=4)
             nc.sync.dma_start(out=t[:], in_=w1_view[:, :, 512 * g : 512 * (g + 1)])
             w1raw.append(t)
         load_z(1)
-        for g in range(2):
-            t = const.tile([P, 4, 512], BF16, name="w2raw%d" % g)
-            nc.sync.dma_start(out=t[:], in_=W2[512 * g : 512 * (g + 1), :].rearrange("(p j) d -> p j d", j=4))
-            w2raw.append(t)
-        for grp in range(2, NG):
-            load_z(grp)
         g1b = const.tile([P, 2, 4], BF16, name="g1b")
         nc.sync.dma_start(out=g1b[:], in_=g1.rearrange("(g p t) -> p g t", g=2, t=4))
         be1b = const.tile([P, 2, 4], BF16, name="be1b")
         nc.sync.dma_start(out=be1b[:], in_=be1.rearrange("(g p t) -> p g t", g=2, t=4))
+        for g in range(2):
+            t = work.tile([P, 4, 512], BF16, name="w2raw", tag="wr", bufs=4)
+            nc.sync.dma_start(out=t[:], in_=W2[512 * g : 512 * (g + 1), :].rearrange("(p j) d -> p j d", j=4))
+            w2raw.append(t)
+        load_z(2)
+        load_z(3)
         b2bc = const.tile([P, D], BF16, name="b2bc")
         nc.sync.dma_start(out=b2bc[:], in_=b2.partition_broadcast(P))
         g2bc = const.tile([P, D], BF16, name="g2bc")
@@ -76,200 +85,208 @@ def tile_emaaggregator_pa_t_kernel(tc, z, W1, b1, g1, be1, W2, b2, g2, be2, out)
         be2bc = const.tile([P, D], BF16, name="be2bc")
         nc.sync.dma_start(out=be2bc[:], in_=be2.partition_broadcast(P))
 
-        neg_half = const.tile([P, GT], F32, name="neg_half")
+        neg_half = const.tile([P, 8], F32, name="neg_half")
         nc.gpsimd.memset(neg_half[:], -0.5)
         warm = const.tile([P, 1], F32, name="warm")
         nc.scalar.activation(out=warm[:], in_=neg_half[:, 0:1], func=ACT.Gelu)
         ident = const.tile([P, P], F32, name="ident")
         make_identity(nc, ident[:])
+        unit = const.tile([P, 8, 2], F32, name="unit")
+        nc.gpsimd.memset(unit[:, 0:8:2, 0:1], -1.0)
+        nc.gpsimd.memset(unit[:, 0:8:2, 1:2], 1.0)
+        nc.gpsimd.memset(unit[:, 1:8:2, 0:1], -1.0 / F)
+        nc.gpsimd.memset(unit[:, 1:8:2, 1:2], 1.0 / F**3)
+        eps_col = const.tile([P, 1], F32, name="eps_col")
+        nc.vector.tensor_scalar(
+            out=eps_col[:], in0=neg_half[:, 0:1], scalar1=0.0, scalar2=EPS, op0=ALU.mult, op1=ALU.add
+        )
 
-        def z_transpose(grp, h):
-            if not ok(grp):
+        acts = []
+        for i in range(NT):
+            acts.append(const.tile([P, F], F32, name="act%d" % i))
+
+        def z_transpose(pr):
+            if not 0 <= pr < NPAIR:
                 return
-            zt = psum.tile([P, 2, 2, P], F32, name="zt", tag="bank", bufs=8)
+            grp, h = divmod(pr, 2)
+            zt = psum.tile([P, 2, 2, P], F32, name="zt", tag="pb", bufs=4)
             for jj in range(2):
                 words = zs[grp][:, 2 * h + jj, :].bitcast(F32)
                 for u in range(2):
                     nc.tensor.transpose(zt[:, jj, u, :], words[:, u:256:2], ident[:])
-            live["zt", grp, h] = zt
+            live["zt", pr] = zt
 
-        def z_copy(grp, h):
-            if not ok(grp):
+        def z_copy(pr):
+            if not 0 <= pr < NPAIR:
                 return
+            grp, h = divmod(pr, 2)
             if h == 0:
-                live["zg", grp] = work.tile([P, GT * P * 4], BF16, name="zg", tag="zg", bufs=2, align_bytes=64)
+                live["zg", grp] = work.tile([P, GT * P * 4], BF16, name="zg", tag="zg", bufs=4, align_bytes=64)
             zgw = live["zg", grp][:].bitcast(F32).rearrange("p (j r u) -> p j r u", j=GT, u=2)
-            nc.scalar.copy(
-                out=zgw[:, 2 * h : 2 * h + 2, :, :], in_=live["zt", grp, h][:].rearrange("p j u r -> p j r u")
-            )
+            nc.scalar.copy(out=zgw[:, 2 * h : 2 * h + 2, :, :], in_=live["zt", pr][:].rearrange("p j u r -> p j r u"))
 
         def z_quantise(grp):
             if not ok(grp):
                 return
-            zc = work.tile([P, GT * P], U32, name="zc", tag="zc", bufs=2, align_bytes=64)
-            zsc = work.tile([P, GT * P], U8, name="zsc", tag="zsc", bufs=2, align_bytes=64)
+            zc = work.tile([P, GT * P], U32, name="zc", tag="codes", bufs=4, align_bytes=64)
+            zsc = work.tile([P, GT * P], U8, name="zsc", tag="scales", bufs=4, align_bytes=64)
             nc.vector.quantize_mx(out=zc[:].bitcast(FP8X4), scales=zsc[:], in_=live["zg", grp][:])
             live["zq", grp] = (zc, zsc)
 
-        def matmul_1(grp, i):
-            if not ok(grp):
+        def matmul_1(i):
+            if not tile_ok(i):
                 return
-            zc, zsc = live["zq", grp]
-            cols = slice(P * i, P * (i + 1))
-            for g in range(2):
-                u = psum.tile([P, 512], BANK_DT, name="u", tag="bank", bufs=8)
-                nc.tensor.matmul_mx(
-                    out=u[:],
-                    lhsT=zc[:, cols].bitcast(FP8X4),
-                    lhsT_scale=zsc[:, cols],
-                    rhs=w1c[g][:].bitcast(FP8X4),
-                    rhs_scale=w1s[g][:],
-                    start=True,
-                    stop=True,
-                )
-                live["u", grp, i, g] = u
-
-        def add_b1(grp, i):
-            if not ok(grp):
-                return
-            x = work.tile([P, F], F32, name="x", tag="x", bufs=2)
-            for g in range(2):
-                half = slice(512 * g, 512 * (g + 1))
-                nc.vector.tensor_tensor(out=x[:, half], in0=live["u", grp, i, g][:], in1=b1p[:, half], op=ALU.add)
-            live["x", grp, i] = x
-
-        def gelu(grp, i):
-            if not ok(grp):
-                return
-            if i == 0:
-                live["sa", grp] = stats.tile([P, GT], F32, name="sa", tag="sa")
-            a = work.tile([P, F], F32, name="a", tag="a", bufs=6)
-            nc.scalar.activation(
-                out=a[:], in_=live["x", grp, i][:], func=ACT.Gelu, accum_out=live["sa", grp][:, i : i + 1]
+            zc, zsc = live["zq", i // GT]
+            cols = slice(P * (i % GT), P * (i % GT + 1))
+            u = psum.tile([P, F], BF16, name="u", tag="pa", bufs=4)
+            nc.tensor.matmul_mx(
+                out=u[:],
+                lhsT=zc[:, cols].bitcast(FP8X4),
+                lhsT_scale=zsc[:, cols],
+                rhs=w1c[:].bitcast(FP8X4),
+                rhs_scale=w1s[:],
+                start=True,
+                stop=True,
             )
-            live["a", grp, i] = a
+            live["u", i] = u
 
-        def square_1(grp, i):
-            if not ok(grp):
+        def add_b1(i):
+            if not tile_ok(i):
                 return
-            if i == 0:
-                live["sq", grp] = stats.tile([P, GT], F32, name="sq", tag="sq")
-            junk = work.tile([P, F], BF16, name="junk", tag="junk", bufs=1)
-            nc.scalar.activation(
-                out=junk[:],
-                in_=live["a", grp, i][:],
-                func=ACT.Square,
-                scale=-float(F),
-                bias=live["sa", grp][:, i : i + 1],
-                accum_out=live["sq", grp][:, i : i + 1],
-            )
+            x = work.tile([P, F], F32, name="x", tag="x", bufs=4)
+            nc.vector.tensor_tensor(out=x[:], in0=live["u", i][:], in1=b1p[:], op=ALU.add)
+            live["x", i] = x
 
-        def neg_mean_1(grp):
-            if not ok(grp):
+        def gelu(i):
+            if not tile_ok(i):
                 return
-            nm = stats.tile([P, GT], F32, name="nm", tag="nm")
-            nc.vector.tensor_scalar(out=nm[:], in0=live["sa", grp][:], scalar1=-1.0 / F, scalar2=None, op0=ALU.mult)
-            live["nm", grp] = nm
-
-        def var_eps_1(grp):
-            if not ok(grp):
-                return
-            ve = stats.tile([P, GT], F32, name="ve", tag="ve")
-            nc.vector.tensor_scalar(
-                out=ve[:], in0=live["sq", grp][:], scalar1=1.0 / F**3, scalar2=EPS, op0=ALU.mult, op1=ALU.add
-            )
-            live["ve", grp] = ve
-
-        def rstd_1(grp):
-            if not ok(grp):
-                return
-            rs = stats.tile([P, GT], F32, name="rs", tag="rs")
-            nc.gpsimd.tensor_tensor(out=rs[:], in0=live["ve", grp][:], in1=neg_half[:], op=ALU.pow)
-            nr = stats.tile([P, GT], F32, name="nr", tag="nr")
-            nc.gpsimd.tensor_tensor(out=nr[:], in0=live["nm", grp][:], in1=rs[:], op=ALU.mult)
-            live["rs", grp] = rs
-            live["nr", grp] = nr
-
-        def normalise(grp, i):
-            if not ok(grp):
-                return
-            col = slice(i, i + 1)
-            xh = work.tile([P, F], F32, name="xh", tag="xh", bufs=4)
-            if i in ON_SCALAR:
+            first, j, count = batch_of[i]
+            if j == 0:
+                live["raw", first] = stats.tile([P, 8, 2], F32, name="raw", tag="raw")
+            if i % 2 == 1:
                 nc.scalar.activation(
-                    out=xh[:],
-                    in_=live["a", grp, i][:],
-                    func=ACT.Identity,
-                    scale=live["rs", grp][:, col],
-                    bias=live["nr", grp][:, col],
+                    out=acts[i][:], in_=live["x", i][:], func=ACT.Gelu, accum_out=live["raw", first][:, j, 0:1]
                 )
             else:
-                nc.vector.tensor_scalar(
-                    out=xh[:],
-                    in0=live["a", grp, i][:],
-                    scalar1=live["nm", grp][:, col],
-                    scalar2=live["rs", grp][:, col],
-                    op0=ALU.add,
-                    op1=ALU.mult,
-                )
-            live["xh", grp, i] = xh
+                nc.scalar.activation(out=acts[i][:], in_=live["x", i][:], func=ACT.Gelu)
 
-        def h_transpose(grp, blk):
+        def stats_1(i):
+            if not tile_ok(i):
+                return
+            first, j, count = batch_of[i]
+            raw = live["raw", first]
+            if i % 2 == 1:
+                junk = work.tile([P, F], BF16, name="junk", tag="junk", bufs=1)
+                nc.scalar.activation(
+                    out=junk[:],
+                    in_=acts[i][:],
+                    func=ACT.Square,
+                    scale=-float(F),
+                    bias=raw[:, j, 0:1],
+                    accum_out=raw[:, j, 1:2],
+                )
+            else:
+                bs = stats.tile([P, 2, 6], F32, name="bs", tag="bs")
+                for c in range(2):
+                    nc.vector.bn_stats(out=bs[:, c, :], in_=acts[i][:, 512 * c : 512 * (c + 1)])
+                nc.vector.bn_aggr(out=raw[:, j, :], in_=bs[:].rearrange("p c s -> p (c s)"))
+
+        def rstd_1(first, count):
+            mv = stats.tile([P, 8, 2], F32, name="mv", tag="mv")
+            nc.gpsimd.tensor_tensor(
+                out=mv[:, 0:count, :], in0=live["raw", first][:, 0:count, :], in1=unit[:, 0:count, :], op=ALU.mult
+            )
+            ve = stats.tile([P, 8], F32, name="ve", tag="ve")
+            nc.gpsimd.tensor_scalar(
+                out=ve[:, 0:count], in0=mv[:, 0:count, 1], scalar1=1.0, scalar2=EPS, op0=ALU.mult, op1=ALU.add
+            )
+            rs = stats.tile([P, 8], F32, name="rs", tag="rs")
+            nc.gpsimd.tensor_tensor(out=rs[:, 0:count], in0=ve[:, 0:count], in1=neg_half[:, 0:count], op=ALU.pow)
+            live["mv", first] = mv
+            live["rs", first] = rs
+
+        def normalise(i):
+            first, j, count = batch_of[i]
+            engine = nc.gpsimd if i < ON_GPSIMD else nc.vector
+            engine.tensor_scalar(
+                out=acts[i][:],
+                in0=acts[i][:],
+                scalar1=live["mv", first][:, j, 0:1],
+                scalar2=live["rs", first][:, j : j + 1],
+                op0=ALU.add,
+                op1=ALU.mult,
+            )
+
+        def h_transpose(n):
+            grp, blk = divmod(n, 8)
             if not ok(grp):
                 return
-            ht = psum.tile([P, GT * P], F32, name="ht", tag="bank", bufs=8)
+            ht = psum.tile([P, GT * P], F32, name="ht", tag="pa", bufs=4)
             for i in range(GT):
-                nc.tensor.transpose(ht[:, P * i : P * (i + 1)], live["xh", grp, i][:, P * blk : P * (blk + 1)], ident[:])
+                nc.tensor.transpose(ht[:, P * i : P * (i + 1)], acts[GT * grp + i][:, P * blk : P * (blk + 1)], ident[:])
             live["ht", grp, blk] = ht
 
         def affine_1(grp, blk):
             if not ok(grp):
                 return
-            if blk == 0:
-                live["hT", grp] = work.tile([P, 8, GT * P], BF16, name="hT", tag="hT", bufs=2)
-            nc.scalar.activation(
-                out=live["hT", grp][:, blk, :],
-                in_=live["ht", grp, blk][:],
-                func=ACT.Identity,
-                scale=g1c[:, blk : blk + 1],
-                bias=be1c[:, blk : blk + 1],
-            )
+            q, t = divmod(blk, 4)
+            if t == 0:
+                live["hT", grp, q] = work.tile([P, 4, GT * P], BF16, name="hT", tag="wr", bufs=4)
+            if grp == 0 and q == 0:
+                nc.vector.tensor_scalar(
+                    out=live["hT", grp, q][:, t, :],
+                    in0=live["ht", grp, blk][:],
+                    scalar1=g1c[:, blk : blk + 1],
+                    scalar2=be1c[:, blk : blk + 1],
+                    op0=ALU.mult,
+                    op1=ALU.add,
+                )
+            else:
+                nc.scalar.activation(
+                    out=live["hT", grp, q][:, t, :],
+                    in_=live["ht", grp, blk][:],
+                    func=ACT.Identity,
+                    scale=g1c[:, blk : blk + 1],
+                    bias=be1c[:, blk : blk + 1],
+                )
 
-        def interleave(grp, g):
+        def interleave(grp, q):
             if not ok(grp):
                 return
-            hg = work.tile([P, GT * P, 4], BF16, name="hg", tag="hg", bufs=2, align_bytes=64)
-            nc.vector.tensor_copy(
-                out=hg[:].rearrange("p (c i) t -> p c t i", i=4),
-                in_=live["hT", grp][:, 4 * g : 4 * g + 4, :].rearrange("p t (c i) -> p c t i", i=4),
-            )
-            live["hg", grp, g] = hg
+            hg = work.tile([P, GT * P, 4], BF16, name="hg", tag="wg", bufs=3, align_bytes=64)
+            dst = hg[:].rearrange("p (c i) t -> p c t i", i=4)
+            src = live["hT", grp, q][:].rearrange("p t (c i) -> p c t i", i=4)
+            if q == 0:
+                nc.vector.tensor_copy(out=dst, in_=src)
+            else:
+                nc.scalar.copy(out=dst, in_=src)
+            live["hg", grp, q] = hg
 
-        def h_quantise(grp, g):
+        def h_quantise(grp, q):
             if not ok(grp):
                 return
-            hc = work.tile([P, GT * P], U32, name="hc", tag="hc", bufs=4, align_bytes=64)
-            hs = work.tile([P, GT * P], U8, name="hs", tag="hs", bufs=4, align_bytes=64)
+            hc = work.tile([P, GT * P], U32, name="hc", tag="codes", bufs=4, align_bytes=64)
+            hs = work.tile([P, GT * P], U8, name="hs", tag="scales", bufs=4, align_bytes=64)
             nc.vector.quantize_mx(
-                out=hc[:].bitcast(FP8X4), scales=hs[:], in_=live["hg", grp, g][:].rearrange("p n t -> p (n t)")
+                out=hc[:].bitcast(FP8X4), scales=hs[:], in_=live["hg", grp, q][:].rearrange("p n t -> p (n t)")
             )
-            live["hq", grp, g] = (hc, hs)
+            live["hq", grp, q] = (hc, hs)
 
         def matmul_2(grp, i):
             if not ok(grp):
                 return
             cols = slice(P * i, P * (i + 1))
-            o = psum.tile([P, D], F32, name="o", tag="bank", bufs=8)
-            for g in range(2):
-                hc, hs = live["hq", grp, g]
+            o = psum.tile([P, D], F32, name="o", tag="pb", bufs=4)
+            for q in range(2):
+                hc, hs = live["hq", grp, q]
                 nc.tensor.matmul_mx(
                     out=o[:],
                     lhsT=hc[:, cols].bitcast(FP8X4),
                     lhsT_scale=hs[:, cols],
-                    rhs=w2c[g][:].bitcast(FP8X4),
-                    rhs_scale=w2s[g][:],
-                    start=(g == 0),
-                    stop=(g == 1),
+                    rhs=w2c[q][:].bitcast(FP8X4),
+                    rhs_scale=w2s[q][:],
+                    start=(q == 0),
+                    stop=(q == 1),
                 )
             live["o", grp, i] = o
 
@@ -278,9 +295,10 @@ def tile_emaaggregator_pa_t_kernel(tc, z, W1, b1, g1, be1, W2, b2, g2, be2, out)
                 return
             if i == 0:
                 live["sy", grp] = stats.tile([P, GT], F32, name="sy", tag="sy")
-            y = work.tile([P, D], F32, name="y", tag="y", bufs=4)
+            if i % 2 == 0:
+                live["y", grp, i // 2] = work.tile([P, 2, D], F32, name="y", tag="zs", bufs=4)
             nc.vector.scalar_tensor_tensor(
-                out=y[:],
+                out=live["y", grp, i // 2][:, i % 2, :],
                 in0=live["o", grp, i][:],
                 scalar=1.0,
                 in1=b2bc[:],
@@ -288,17 +306,16 @@ def tile_emaaggregator_pa_t_kernel(tc, z, W1, b1, g1, be1, W2, b2, g2, be2, out)
                 op1=ALU.add,
                 accum_out=live["sy", grp][:, i : i + 1],
             )
-            live["y", grp, i] = y
 
         def square_2(grp, i):
             if not ok(grp):
                 return
             if i == 0:
                 live["sq2", grp] = stats.tile([P, GT], F32, name="sq2", tag="sq2")
-            junk2 = work.tile([P, D], BF16, name="junk2", tag="junk2", bufs=1)
+            junk2 = work.tile([P, D], BF16, name="junk2", tag="junk", bufs=1)
             nc.scalar.activation(
                 out=junk2[:],
-                in_=live["y", grp, i][:],
+                in_=live["y", grp, i // 2][:, i % 2, :],
                 func=ACT.Square,
                 scale=-float(D),
                 bias=live["sy", grp][:, i : i + 1],
@@ -312,75 +329,67 @@ def tile_emaaggregator_pa_t_kernel(tc, z, W1, b1, g1, be1, W2, b2, g2, be2, out)
             nc.vector.tensor_scalar(out=nm2[:], in0=live["sy", grp][:], scalar1=-1.0 / D, scalar2=None, op0=ALU.mult)
             live["nm2", grp] = nm2
 
-        def var_eps_2(grp):
-            if not ok(grp):
-                return
-            ve2 = stats.tile([P, GT], F32, name="ve2", tag="ve2")
-            nc.vector.tensor_scalar(
-                out=ve2[:], in0=live["sq2", grp][:], scalar1=1.0 / D**3, scalar2=EPS, op0=ALU.mult, op1=ALU.add
-            )
-            live["ve2", grp] = ve2
-
         def rstd_2(grp):
             if not ok(grp):
                 return
             rs2 = stats.tile([P, GT], F32, name="rs2", tag="rs2")
-            nc.gpsimd.tensor_tensor(out=rs2[:], in0=live["ve2", grp][:], in1=neg_half[:], op=ALU.pow)
+            nc.scalar.activation(
+                out=rs2[:], in_=live["sq2", grp][:], func=ACT.Abs_reciprocal_sqrt, scale=1.0 / D**3, bias=eps_col[:, 0:1]
+            )
             live["rs2", grp] = rs2
 
         def centre_gain(grp, i):
             if not ok(grp):
                 return
-            q = work.tile([P, D], F32, name="q", tag="q", bufs=4)
+            if i % 2 == 0:
+                live["q", grp, i // 2] = work.tile([P, 2, D], F32, name="q", tag="x", bufs=4)
             nc.vector.scalar_tensor_tensor(
-                out=q[:],
-                in0=live["y", grp, i][:],
+                out=live["q", grp, i // 2][:, i % 2, :],
+                in0=live["y", grp, i // 2][:, i % 2, :],
                 scalar=live["nm2", grp][:, i : i + 1],
                 in1=g2bc[:],
                 op0=ALU.add,
                 op1=ALU.mult,
             )
-            live["q", grp, i] = q
 
         def scale_shift(grp, i):
             if not ok(grp):
                 return
-            ot = work.tile([P, D], F32, name="ot", tag="ot", bufs=4)
+            if i % 2 == 0:
+                live["ot", grp, i // 2] = work.tile([P, 2, D], F32, name="ot", tag="zg", bufs=4, align_bytes=64)
             nc.vector.scalar_tensor_tensor(
-                out=ot[:],
-                in0=live["q", grp, i][:],
+                out=live["ot", grp, i // 2][:, i % 2, :],
+                in0=live["q", grp, i // 2][:, i % 2, :],
                 scalar=live["rs2", grp][:, i : i + 1],
                 in1=be2bc[:],
                 op0=ALU.mult,
                 op1=ALU.add,
             )
-            live["ot", grp, i] = ot
 
-        def store(grp, i):
+        def store(grp, half):
             if not ok(grp):
                 return
-            nc.sync.dma_start(out=out_view[:, GT * grp + i, :], in_=live["ot", grp, i][:])
+            first = GT * grp + 2 * half
+            nc.sync.dma_start(out=out_view[:, first : first + 2, :], in_=live["ot", grp, half][:])
 
-        z_transpose(0, 0)
+        z_transpose(0)
         w1g = []
         for g in range(2):
-            w1g.append(const.tile([P, 2048], BF16, name="w1g%d" % g, align_bytes=64))
+            w1g.append(work.tile([P, 2048], BF16, name="w1g", tag="wg", bufs=3, align_bytes=64))
         dst = [w1g[g][:].rearrange("p (t m j) -> p t m j", t=4, j=4) for g in range(2)]
         src = [w1raw[g][:].rearrange("p j (m t) -> p t m j", t=4) for g in range(2)]
-        w1c, w1s, w2c, w2s = [], [], [], []
-        for g in range(2):
-            w1c.append(const.tile([P, 512], U32, name="w1c%d" % g, align_bytes=64))
-            w1s.append(const.tile([P, 512], U8, name="w1s%d" % g, align_bytes=64))
+        w1c = const.tile([P, F], U32, name="w1c", align_bytes=64)
+        w1s = const.tile([P, F], U8, name="w1s", align_bytes=64)
         nc.vector.tensor_copy(out=dst[0][:, 0:2], in_=src[0][:, 0:2])
         nc.vector.tensor_copy(out=dst[0][:, 2:4], in_=src[0][:, 2:4])
         nc.scalar.copy(out=dst[1][:, 2:4], in_=src[1][:, 2:4])
-        z_copy(0, 0)
-        z_transpose(0, 1)
-        z_copy(0, 1)
+        z_copy(0)
+        z_transpose(1)
+        z_copy(1)
         nc.vector.tensor_copy(out=dst[1][:, 0:2], in_=src[1][:, 0:2])
-        nc.vector.quantize_mx(out=w1c[0][:].bitcast(FP8X4), scales=w1s[0][:], in_=w1g[0][:])
+        nc.vector.quantize_mx(out=w1c[:, 0:512].bitcast(FP8X4), scales=w1s[:, 0:512], in_=w1g[0][:])
         z_quantise(0)
-        nc.vector.quantize_mx(out=w1c[1][:].bitcast(FP8X4), scales=w1s[1][:], in_=w1g[1][:])
+        nc.vector.quantize_mx(out=w1c[:, 512:1024].bitcast(FP8X4), scales=w1s[:, 512:1024], in_=w1g[1][:])
         b1p = const.tile([P, F], BF16, name="b1p")
         nc.scalar.copy(
             out=b1p[:].rearrange("p (g t m) -> p g t m", g=2, t=4),
@@ -390,12 +399,25 @@ def tile_emaaggregator_pa_t_kernel(tc, z, W1, b1, g1, be1, W2, b2, g2, be2, out)
         nc.gpsimd.tensor_copy(out=g1c[:], in_=g1b[:].rearrange("p g t -> p (g t)"))
         be1c = const.tile([P, 8], F32, name="be1c")
         nc.gpsimd.tensor_copy(out=be1c[:], in_=be1b[:].rearrange("p g t -> p (g t)"))
+        z_transpose(2)
+        z_transpose(3)
+        z_copy(2)
+        matmul_1(0)
 
-        def prep_w2():
-            w2g = []
-            for g in range(2):
-                w2g.append(const.tile([P, 512, 4], BF16, name="w2g%d" % g, align_bytes=64))
-                nc.vector.tensor_copy(out=w2g[g][:], in_=w2raw[g][:].rearrange("p j d -> p d j"))
+        w2g = []
+        w2c, w2s = [], []
+        for g in range(2):
+            w2g.append(work.tile([P, 512, 4], BF16, name="w2g", tag="wg", bufs=3, align_bytes=64))
+            nc.gpsimd.tensor_scalar(
+                out=w2g[g][:],
+                in0=w2raw[g][:].rearrange("p j d -> p d j"),
+                scalar1=1.0,
+                scalar2=0.0,
+                op0=ALU.mult,
+                op1=ALU.add,
+            )
+
+        def quantise_w2():
             for g in range(2):
                 w2c.append(const.tile([P, 512], U32, name="w2c%d" % g, align_bytes=64))
                 w2s.append(const.tile([P, 512], U8, name="w2s%d" % g, align_bytes=64))
@@ -403,82 +425,64 @@ def tile_emaaggregator_pa_t_kernel(tc, z, W1, b1, g1, be1, W2, b2, g2, be2, out)
                     out=w2c[g][:].bitcast(FP8X4), scales=w2s[g][:], in_=w2g[g][:].rearrange("p d j -> p (d j)")
                 )
 
-        for step in range(NG + 2):
-            if True:
-                z_transpose(step + 1, 0)
-                matmul_1(step, 0)
-                matmul_1(step, 1)
-                z_transpose(step + 1, 1)
-                matmul_1(step, 2)
-                var_eps_1(step - 1)
-                neg_mean_1(step - 1)
-                add_b1(step, 0)
-                rstd_1(step - 1)
-                normalise(step - 1, 0)
-                normalise(step - 1, 1)
-                z_copy(step + 1, 0)
-                normalise(step - 1, 2)
-                normalise(step - 1, 3)
-                h_transpose(step - 1, 0)
-                centre_gain(step - 2, 0)
-                gelu(step, 0)
-                var_eps_2(step - 2)
-                centre_gain(step - 2, 1)
-                h_transpose(step - 1, 1)
-                rstd_2(step - 2)
-                add_b1(step, 1)
-                h_transpose(step - 1, 2)
-                z_copy(step + 1, 1)
-                h_transpose(step - 1, 3)
-                affine_1(step - 1, 0)
-                add_b1(step, 2)
-                h_transpose(step - 1, 4)
-                affine_1(step - 1, 1)
-                h_transpose(step - 1, 5)
-                h_transpose(step - 1, 6)
-                affine_1(step - 1, 2)
-                z_quantise(step + 1)
-                h_transpose(step - 1, 7)
-                affine_1(step - 1, 3)
-                centre_gain(step - 2, 2)
-                matmul_1(step, 3)
-                affine_1(step - 1, 4)
-                interleave(step - 1, 0)
-                affine_1(step - 1, 5)
-                affine_1(step - 1, 6)
-                centre_gain(step - 2, 3)
-                affine_1(step - 1, 7)
-                h_quantise(step - 1, 0)
-                gelu(step, 1)
-                interleave(step - 1, 1)
-                square_1(step, 0)
-                h_quantise(step - 1, 1)
-                matmul_2(step - 1, 0)
-                square_1(step, 1)
-                add_b1(step, 3)
-                matmul_2(step - 1, 1)
-                gelu(step, 2)
-                scale_shift(step - 2, 0)
-                matmul_2(step - 1, 2)
-                scale_shift(step - 2, 1)
-                store(step - 2, 0)
-                matmul_2(step - 1, 3)
-                square_1(step, 2)
-                scale_shift(step - 2, 2)
-                store(step - 2, 1)
-                add_b2(step - 1, 0)
-                store(step - 2, 2)
-                gelu(step, 3)
-                add_b2(step - 1, 1)
-                add_b2(step - 1, 2)
-                square_1(step, 3)
-                add_b2(step - 1, 3)
-                scale_shift(step - 2, 3)
-                square_2(step - 1, 0)
-                neg_mean_2(step - 1)
-                square_2(step - 1, 1)
-                store(step - 2, 3)
-                square_2(step - 1, 2)
-                square_2(step - 1, 3)
-            if step == 0:
-                prep_w2()
+        late_loads = {0: [4, 5], 4: [6], 8: [7]}
+        batch_end = {}
+        for first, count in BATCHES:
+            batch_end[first + count - 1] = (first, count)
+        for t in range(NT + 2):
+            for grp in late_loads.get(t, []):
+                load_z(grp)
+            if t % 2 == 0:
+                z_transpose(t // 2 + 4)
+            matmul_1(t + 1)
+            add_b1(t)
+            if t % 2 == 0:
+                z_copy(t // 2 + 3)
+            gelu(t - 1)
+            stats_1(t - 2)
+            if t % 4 == 1:
+                z_quantise((t + 3) // 4)
+            if t == 8:
+                quantise_w2()
+            if t == NT:
+                for n in range(4):
+                    h_transpose(n)
+            if t - 2 in batch_end:
+                first, count = batch_end[t - 2]
+                rstd_1(first, count)
+                for j in range(count):
+                    if first + j < ON_GPSIMD:
+                        normalise(first + j)
+
+        for s in range(NG + 2):
+            for i in range(GT):
+                add_b2(s - 1, i)
+            neg_mean_2(s - 1)
+            for blk in range(4):
+                affine_1(s, blk)
+                h_transpose(8 * s + blk + 4)
+            interleave(s, 0)
+            for blk in range(4, 8):
+                affine_1(s, blk)
+                h_transpose(8 * s + blk + 4)
+            centre_gain(s - 1, 0)
+            centre_gain(s - 1, 1)
+            h_quantise(s, 0)
+            centre_gain(s - 1, 2)
+            centre_gain(s - 1, 3)
+            interleave(s, 1)
+            h_quantise(s, 1)
+            for i in range(GT):
+                matmul_2(s, i)
+            if s == 1:
+                for i in range(ON_GPSIMD, NT):
+                    normalise(i)
+            scale_shift(s - 2, 0)
+            scale_shift(s - 2, 1)
+            store(s - 2, 0)
+            scale_shift(s - 2, 2)
+            scale_shift(s - 2, 3)
+            store(s - 2, 1)
+            for i in range(GT):
+                square_2(s - 1, i)
+            rstd_2(s - 1)

@@ -20,8 +20,11 @@ NT = B // P
 GT = 4
 NG = NT // GT
 NPAIR = NT // 2
-BATCHES = [(0, 8), (8, 8), (16, 8), (24, 4), (28, 4)]
+BATCHES = [(4 * b, 4) for b in range(8)]
 ON_GPSIMD = 28
+SIZES = [4, 4, 4, 4, 4, 4, 4, 2, 2]
+STARTS = [sum(SIZES[:g]) for g in range(len(SIZES))]
+NH = len(SIZES)
 
 
 def tile_emaaggregator_pa_t_kernel(tc, z, W1, b1, g1, be1, W2, b2, g2, be2, out):
@@ -43,6 +46,12 @@ def tile_emaaggregator_pa_t_kernel(tc, z, W1, b1, g1, be1, W2, b2, g2, be2, out)
 
         def tile_ok(i):
             return 0 <= i < NT
+
+        def okh(grp):
+            return 0 <= grp < NH
+
+        def size(grp):
+            return SIZES[grp] if okh(grp) else 0
 
         batch_of = {}
         for first, count in BATCHES:
@@ -219,19 +228,21 @@ def tile_emaaggregator_pa_t_kernel(tc, z, W1, b1, g1, be1, W2, b2, g2, be2, out)
 
         def h_transpose(n):
             grp, blk = divmod(n, 8)
-            if not ok(grp):
+            if not okh(grp):
                 return
-            ht = psum.tile([P, GT * P], F32, name="ht", tag="pa", bufs=4)
-            for i in range(GT):
-                nc.tensor.transpose(ht[:, P * i : P * (i + 1)], acts[GT * grp + i][:, P * blk : P * (blk + 1)], ident[:])
+            ht = psum.tile([P, SIZES[grp] * P], F32, name="ht", tag="pa", bufs=4)
+            for i in range(SIZES[grp]):
+                nc.tensor.transpose(
+                    ht[:, P * i : P * (i + 1)], acts[STARTS[grp] + i][:, P * blk : P * (blk + 1)], ident[:]
+                )
             live["ht", grp, blk] = ht
 
         def affine_1(grp, blk):
-            if not ok(grp):
+            if not okh(grp):
                 return
             q, t = divmod(blk, 4)
             if t == 0:
-                live["hT", grp, q] = work.tile([P, 4, GT * P], BF16, name="hT", tag="wr", bufs=4)
+                live["hT", grp, q] = work.tile([P, 4, SIZES[grp] * P], BF16, name="hT", tag="wr", bufs=4)
             if grp == 0 and q == 0:
                 nc.vector.tensor_scalar(
                     out=live["hT", grp, q][:, t, :],
@@ -251,29 +262,29 @@ def tile_emaaggregator_pa_t_kernel(tc, z, W1, b1, g1, be1, W2, b2, g2, be2, out)
                 )
 
         def interleave(grp, q):
-            if not ok(grp):
+            if not okh(grp):
                 return
-            hg = work.tile([P, GT * P, 4], BF16, name="hg", tag="wg", bufs=3, align_bytes=64)
+            hg = work.tile([P, SIZES[grp] * P, 4], BF16, name="hg", tag="wg", bufs=3, align_bytes=64)
             dst = hg[:].rearrange("p (c i) t -> p c t i", i=4)
             src = live["hT", grp, q][:].rearrange("p t (c i) -> p c t i", i=4)
-            if q == 0:
+            if q == 0 or grp == 0:
                 nc.vector.tensor_copy(out=dst, in_=src)
             else:
                 nc.scalar.copy(out=dst, in_=src)
             live["hg", grp, q] = hg
 
         def h_quantise(grp, q):
-            if not ok(grp):
+            if not okh(grp):
                 return
-            hc = work.tile([P, GT * P], U32, name="hc", tag="codes", bufs=4, align_bytes=64)
-            hs = work.tile([P, GT * P], U8, name="hs", tag="scales", bufs=4, align_bytes=64)
+            hc = work.tile([P, SIZES[grp] * P], U32, name="hc", tag="codes", bufs=4, align_bytes=64)
+            hs = work.tile([P, SIZES[grp] * P], U8, name="hs", tag="scales", bufs=4, align_bytes=64)
             nc.vector.quantize_mx(
                 out=hc[:].bitcast(FP8X4), scales=hs[:], in_=live["hg", grp, q][:].rearrange("p n t -> p (n t)")
             )
             live["hq", grp, q] = (hc, hs)
 
         def matmul_2(grp, i):
-            if not ok(grp):
+            if not okh(grp):
                 return
             cols = slice(P * i, P * (i + 1))
             o = psum.tile([P, D], F32, name="o", tag="pb", bufs=4)
@@ -291,7 +302,7 @@ def tile_emaaggregator_pa_t_kernel(tc, z, W1, b1, g1, be1, W2, b2, g2, be2, out)
             live["o", grp, i] = o
 
         def add_b2(grp, i):
-            if not ok(grp):
+            if not okh(grp):
                 return
             if i == 0:
                 live["sy", grp] = stats.tile([P, GT], F32, name="sy", tag="sy")
@@ -308,7 +319,7 @@ def tile_emaaggregator_pa_t_kernel(tc, z, W1, b1, g1, be1, W2, b2, g2, be2, out)
             )
 
         def square_2(grp, i):
-            if not ok(grp):
+            if not okh(grp):
                 return
             if i == 0:
                 live["sq2", grp] = stats.tile([P, GT], F32, name="sq2", tag="sq2")
@@ -323,23 +334,31 @@ def tile_emaaggregator_pa_t_kernel(tc, z, W1, b1, g1, be1, W2, b2, g2, be2, out)
             )
 
         def neg_mean_2(grp):
-            if not ok(grp):
+            if not okh(grp):
                 return
             nm2 = stats.tile([P, GT], F32, name="nm2", tag="nm2")
-            nc.vector.tensor_scalar(out=nm2[:], in0=live["sy", grp][:], scalar1=-1.0 / D, scalar2=None, op0=ALU.mult)
+            n = SIZES[grp]
+            nc.vector.tensor_scalar(
+                out=nm2[:, 0:n], in0=live["sy", grp][:, 0:n], scalar1=-1.0 / D, scalar2=None, op0=ALU.mult
+            )
             live["nm2", grp] = nm2
 
         def rstd_2(grp):
-            if not ok(grp):
+            if not okh(grp):
                 return
             rs2 = stats.tile([P, GT], F32, name="rs2", tag="rs2")
+            n = SIZES[grp]
             nc.scalar.activation(
-                out=rs2[:], in_=live["sq2", grp][:], func=ACT.Abs_reciprocal_sqrt, scale=1.0 / D**3, bias=eps_col[:, 0:1]
+                out=rs2[:, 0:n],
+                in_=live["sq2", grp][:, 0:n],
+                func=ACT.Abs_reciprocal_sqrt,
+                scale=1.0 / D**3,
+                bias=eps_col[:, 0:1],
             )
             live["rs2", grp] = rs2
 
         def centre_gain(grp, i):
-            if not ok(grp):
+            if not okh(grp):
                 return
             if i % 2 == 0:
                 live["q", grp, i // 2] = work.tile([P, 2, D], F32, name="q", tag="x", bufs=4)
@@ -353,7 +372,7 @@ def tile_emaaggregator_pa_t_kernel(tc, z, W1, b1, g1, be1, W2, b2, g2, be2, out)
             )
 
         def scale_shift(grp, i):
-            if not ok(grp):
+            if not okh(grp):
                 return
             if i % 2 == 0:
                 live["ot", grp, i // 2] = work.tile([P, 2, D], F32, name="ot", tag="zg", bufs=4, align_bytes=64)
@@ -367,9 +386,9 @@ def tile_emaaggregator_pa_t_kernel(tc, z, W1, b1, g1, be1, W2, b2, g2, be2, out)
             )
 
         def store(grp, half):
-            if not ok(grp):
+            if not okh(grp):
                 return
-            first = GT * grp + 2 * half
+            first = STARTS[grp] + 2 * half
             nc.sync.dma_start(out=out_view[:, first : first + 2, :], in_=live["ot", grp, half][:])
 
         z_transpose(0)
@@ -388,8 +407,16 @@ def tile_emaaggregator_pa_t_kernel(tc, z, W1, b1, g1, be1, W2, b2, g2, be2, out)
         z_copy(1)
         nc.vector.tensor_copy(out=dst[1][:, 0:2], in_=src[1][:, 0:2])
         nc.vector.quantize_mx(out=w1c[:, 0:512].bitcast(FP8X4), scales=w1s[:, 0:512], in_=w1g[0][:])
-        z_quantise(0)
         nc.vector.quantize_mx(out=w1c[:, 512:1024].bitcast(FP8X4), scales=w1s[:, 512:1024], in_=w1g[1][:])
+        z_quantise(0)
+        go = [const.tile([P, 1], F32, name="go%d" % g) for g in range(2)]
+
+        def let_go(g):
+            nc.vector.tensor_scalar(
+                out=go[g][:], in0=neg_half[:, 0:1], scalar1=0.0, scalar2=1.0, op0=ALU.mult, op1=ALU.add
+            )
+
+        let_go(0)
         b1p = const.tile([P, F], BF16, name="b1p")
         nc.scalar.copy(
             out=b1p[:].rearrange("p (g t m) -> p g t m", g=2, t=4),
@@ -406,16 +433,19 @@ def tile_emaaggregator_pa_t_kernel(tc, z, W1, b1, g1, be1, W2, b2, g2, be2, out)
 
         w2g = []
         w2c, w2s = [], []
-        for g in range(2):
+
+        def group_w2(g):
             w2g.append(work.tile([P, 512, 4], BF16, name="w2g", tag="wg", bufs=3, align_bytes=64))
             nc.gpsimd.tensor_scalar(
                 out=w2g[g][:],
                 in0=w2raw[g][:].rearrange("p j d -> p d j"),
-                scalar1=1.0,
+                scalar1=go[g][:, 0:1],
                 scalar2=0.0,
                 op0=ALU.mult,
                 op1=ALU.add,
             )
+
+        group_w2(0)
 
         def quantise_w2():
             for g in range(2):
@@ -442,7 +472,10 @@ def tile_emaaggregator_pa_t_kernel(tc, z, W1, b1, g1, be1, W2, b2, g2, be2, out)
             stats_1(t - 2)
             if t % 4 == 1:
                 z_quantise((t + 3) // 4)
-            if t == 8:
+            if t == 1:
+                let_go(1)
+                group_w2(1)
+            if t == 4:
                 quantise_w2()
             if t == NT:
                 for n in range(4):
@@ -454,8 +487,8 @@ def tile_emaaggregator_pa_t_kernel(tc, z, W1, b1, g1, be1, W2, b2, g2, be2, out)
                     if first + j < ON_GPSIMD:
                         normalise(first + j)
 
-        for s in range(NG + 2):
-            for i in range(GT):
+        for s in range(NH + 2):
+            for i in range(size(s - 1)):
                 add_b2(s - 1, i)
             neg_mean_2(s - 1)
             for blk in range(4):
@@ -465,24 +498,22 @@ def tile_emaaggregator_pa_t_kernel(tc, z, W1, b1, g1, be1, W2, b2, g2, be2, out)
             for blk in range(4, 8):
                 affine_1(s, blk)
                 h_transpose(8 * s + blk + 4)
-            centre_gain(s - 1, 0)
-            centre_gain(s - 1, 1)
+            for i in range(size(s - 1) // 2):
+                centre_gain(s - 1, i)
             h_quantise(s, 0)
-            centre_gain(s - 1, 2)
-            centre_gain(s - 1, 3)
+            for i in range(size(s - 1) // 2, size(s - 1)):
+                centre_gain(s - 1, i)
             interleave(s, 1)
             h_quantise(s, 1)
-            for i in range(GT):
+            for i in range(size(s)):
                 matmul_2(s, i)
             if s == 1:
                 for i in range(ON_GPSIMD, NT):
                     normalise(i)
-            scale_shift(s - 2, 0)
-            scale_shift(s - 2, 1)
-            store(s - 2, 0)
-            scale_shift(s - 2, 2)
-            scale_shift(s - 2, 3)
-            store(s - 2, 1)
-            for i in range(GT):
+            for i in range(size(s - 2)):
+                scale_shift(s - 2, i)
+                if i % 2 == 1:
+                    store(s - 2, i // 2)
+            for i in range(size(s - 1)):
                 square_2(s - 1, i)
             rstd_2(s - 1)

@@ -198,7 +198,13 @@ def tile_emaaggregator_pa_t_kernel(tc, z, W1, b1, g1, be1, W2, b2, g2, be2, out)
                 bs = stats.tile([P, 2, 6], F32, name="bs", tag="bs")
                 for c in range(2):
                     nc.vector.bn_stats(out=bs[:, c, :], in_=acts[i][:, 512 * c : 512 * (c + 1)])
-                nc.vector.bn_aggr(out=raw[:, j, :], in_=bs[:].rearrange("p c s -> p (c s)"))
+                live["bs", i] = bs
+
+        def aggregate_1(i):
+            if not tile_ok(i) or i % 2 == 1:
+                return
+            first, j, count = batch_of[i]
+            nc.vector.bn_aggr(out=live["raw", first][:, j, :], in_=live["bs", i][:].rearrange("p c s -> p (c s)"))
 
         def rstd_1(first, count):
             mv = stats.tile([P, 8, 2], F32, name="mv", tag="mv")
@@ -459,13 +465,14 @@ def tile_emaaggregator_pa_t_kernel(tc, z, W1, b1, g1, be1, W2, b2, g2, be2, out)
         batch_end = {}
         for first, count in BATCHES:
             batch_end[first + count - 1] = (first, count)
-        for t in range(NT + 2):
+        for t in range(NT + 3):
             for grp in late_loads.get(t, []):
                 load_z(grp)
             if t % 2 == 0:
                 z_transpose(t // 2 + 4)
             matmul_1(t + 1)
             add_b1(t)
+            aggregate_1(t - 3)
             if t % 2 == 0:
                 z_copy(t // 2 + 3)
             gelu(t - 1)
@@ -490,11 +497,14 @@ def tile_emaaggregator_pa_t_kernel(tc, z, W1, b1, g1, be1, W2, b2, g2, be2, out)
         for s in range(NH + 2):
             for i in range(size(s - 1)):
                 add_b2(s - 1, i)
-            neg_mean_2(s - 1)
             for blk in range(4):
                 affine_1(s, blk)
+                if blk == 0:
+                    rstd_2(s - 2)
                 h_transpose(8 * s + blk + 4)
             interleave(s, 0)
+            neg_mean_2(s - 1)
+            scale_shift(s - 2, 0)
             for blk in range(4, 8):
                 affine_1(s, blk)
                 h_transpose(8 * s + blk + 4)
@@ -510,10 +520,9 @@ def tile_emaaggregator_pa_t_kernel(tc, z, W1, b1, g1, be1, W2, b2, g2, be2, out)
             if s == 1:
                 for i in range(ON_GPSIMD, NT):
                     normalise(i)
-            for i in range(size(s - 2)):
+            for i in range(1, size(s - 2)):
                 scale_shift(s - 2, i)
                 if i % 2 == 1:
                     store(s - 2, i // 2)
             for i in range(size(s - 1)):
                 square_2(s - 1, i)
-            rstd_2(s - 1)

@@ -494,35 +494,41 @@ def tile_emaaggregator_pa_t_kernel(tc, z, W1, b1, g1, be1, W2, b2, g2, be2, out)
                     if first + j < ON_GPSIMD:
                         normalise(first + j)
 
+        for blk in range(4):
+            affine_1(0, blk)
+            h_transpose(blk + 4)
+        interleave(0, 0)
         for s in range(NH + 2):
             for i in range(size(s - 1)):
                 add_b2(s - 1, i)
-            for blk in range(4):
-                affine_1(s, blk)
-                if blk == 0:
-                    rstd_2(s - 2)
-                h_transpose(8 * s + blk + 4)
-            interleave(s, 0)
-            neg_mean_2(s - 1)
-            scale_shift(s - 2, 0)
             for blk in range(4, 8):
                 affine_1(s, blk)
+                if blk == 4:
+                    rstd_2(s - 2)
                 h_transpose(8 * s + blk + 4)
+            scale_shift(s - 2, 0)
+            neg_mean_2(s - 1)
+            scale_shift(s - 2, 1)
+            store(s - 2, 0)
+            interleave(s, 1)
             for i in range(size(s - 1) // 2):
                 centre_gain(s - 1, i)
             h_quantise(s, 0)
             for i in range(size(s - 1) // 2, size(s - 1)):
                 centre_gain(s - 1, i)
-            interleave(s, 1)
+            for blk in range(4):
+                affine_1(s + 1, blk)
+                h_transpose(8 * (s + 1) + blk + 4)
             h_quantise(s, 1)
             for i in range(size(s)):
                 matmul_2(s, i)
             if s == 1:
                 for i in range(ON_GPSIMD, NT):
                     normalise(i)
-            for i in range(1, size(s - 2)):
+            for i in range(2, size(s - 2)):
                 scale_shift(s - 2, i)
                 if i % 2 == 1:
                     store(s - 2, i // 2)
+            interleave(s + 1, 0)
             for i in range(size(s - 1)):
                 square_2(s - 1, i)

@@ -58,8 +58,11 @@ def tile_emaaggregator_pa_t_kernel(tc, z, W1, b1, g1, be1, W2, b2, g2, be2, out)
             for j in range(count):
                 batch_of[first + j] = (first, j, count)
 
-        b1n = work.tile([P, F], BF16, name="b1n", tag="x", bufs=4)
-        nc.scalar.dma_start(out=b1n[:], in_=b1.partition_broadcast(P))
+        b1row = work.tile([P, F], BF16, name="b1row", tag="x", bufs=4)
+        nc.vector.memset(b1row[:], 0.0)
+        nc.scalar.dma_start(out=b1row[0:1, :], in_=b1.rearrange("(o f) -> o f", o=1))
+        ones = const.tile([P, P], BF16, name="ones")
+        nc.vector.memset(ones[:], 1.0)
 
         zs = {}
 
@@ -70,29 +73,30 @@ def tile_emaaggregator_pa_t_kernel(tc, z, W1, b1, g1, be1, W2, b2, g2, be2, out)
 
         w1raw = []
         w2raw = []
-        load_z(0)
         w1_view = W1.rearrange("(p j) c -> p j c", j=4)
         for g in range(2):
             t = work.tile([P, 4, 512], BF16, name="w1raw", tag="wr", bufs=4)
             nc.sync.dma_start(out=t[:], in_=w1_view[:, :, 512 * g : 512 * (g + 1)])
             w1raw.append(t)
-        load_z(1)
-        g1b = const.tile([P, 2, 4], BF16, name="g1b")
-        nc.sync.dma_start(out=g1b[:], in_=g1.rearrange("(g p t) -> p g t", g=2, t=4))
-        be1b = const.tile([P, 2, 4], BF16, name="be1b")
-        nc.sync.dma_start(out=be1b[:], in_=be1.rearrange("(g p t) -> p g t", g=2, t=4))
+            load_z(g)
         for g in range(2):
             t = work.tile([P, 4, 512], BF16, name="w2raw", tag="wr", bufs=4)
             nc.sync.dma_start(out=t[:], in_=W2[512 * g : 512 * (g + 1), :].rearrange("(p j) d -> p j d", j=4))
             w2raw.append(t)
         load_z(2)
         load_z(3)
+        g1b = const.tile([P, 2, 4], BF16, name="g1b")
+        nc.sync.dma_start(out=g1b[:], in_=g1.rearrange("(g p t) -> p g t", g=2, t=4))
+        be1b = const.tile([P, 2, 4], BF16, name="be1b")
+        nc.sync.dma_start(out=be1b[:], in_=be1.rearrange("(g p t) -> p g t", g=2, t=4))
         b2bc = const.tile([P, D], BF16, name="b2bc")
-        nc.sync.dma_start(out=b2bc[:], in_=b2.partition_broadcast(P))
         g2bc = const.tile([P, D], BF16, name="g2bc")
-        nc.sync.dma_start(out=g2bc[:], in_=g2.partition_broadcast(P))
         be2bc = const.tile([P, D], BF16, name="be2bc")
-        nc.sync.dma_start(out=be2bc[:], in_=be2.partition_broadcast(P))
+
+        def load_second_norm():
+            nc.sync.dma_start(out=b2bc[:], in_=b2.partition_broadcast(P))
+            nc.sync.dma_start(out=g2bc[:], in_=g2.partition_broadcast(P))
+            nc.sync.dma_start(out=be2bc[:], in_=be2.partition_broadcast(P))
 
         neg_half = const.tile([P, 8], F32, name="neg_half")
         nc.gpsimd.memset(neg_half[:], -0.5)
@@ -410,6 +414,10 @@ def tile_emaaggregator_pa_t_kernel(tc, z, W1, b1, g1, be1, W2, b2, g2, be2, out)
         nc.scalar.copy(out=dst[1][:, 2:4], in_=src[1][:, 2:4])
         z_copy(0)
         z_transpose(1)
+        b1ps = []
+        for g in range(2):
+            b1ps.append(psum.tile([P, 512], F32, name="b1ps", tag="pa", bufs=4))
+            nc.tensor.matmul(out=b1ps[g][:], lhsT=ones[:], rhs=b1row[:, 512 * g : 512 * (g + 1)], start=True, stop=True)
         z_copy(1)
         nc.vector.tensor_copy(out=dst[1][:, 0:2], in_=src[1][:, 0:2])
         nc.vector.quantize_mx(out=w1c[:, 0:512].bitcast(FP8X4), scales=w1s[:, 0:512], in_=w1g[0][:])
@@ -424,17 +432,13 @@ def tile_emaaggregator_pa_t_kernel(tc, z, W1, b1, g1, be1, W2, b2, g2, be2, out)
 
         let_go(0)
         b1p = const.tile([P, F], BF16, name="b1p")
-        nc.scalar.copy(
-            out=b1p[:].rearrange("p (g t m) -> p g t m", g=2, t=4),
-            in_=b1n[:].rearrange("p (g m t) -> p g t m", g=2, t=4),
-        )
+        for g in range(2):
+            nc.scalar.copy(
+                out=b1p[:, 512 * g : 512 * (g + 1)].rearrange("p (t m) -> p t m", t=4),
+                in_=b1ps[g][:].rearrange("p (m t) -> p t m", t=4),
+            )
         g1c = const.tile([P, 8], F32, name="g1c")
-        nc.gpsimd.tensor_copy(out=g1c[:], in_=g1b[:].rearrange("p g t -> p (g t)"))
         be1c = const.tile([P, 8], F32, name="be1c")
-        nc.gpsimd.tensor_copy(out=be1c[:], in_=be1b[:].rearrange("p g t -> p (g t)"))
-        z_transpose(2)
-        z_transpose(3)
-        z_copy(2)
         matmul_1(0)
 
         w2g = []
@@ -468,20 +472,28 @@ def tile_emaaggregator_pa_t_kernel(tc, z, W1, b1, g1, be1, W2, b2, g2, be2, out)
         for t in range(NT + 3):
             for grp in late_loads.get(t, []):
                 load_z(grp)
-            if t % 2 == 0:
-                z_transpose(t // 2 + 4)
             matmul_1(t + 1)
+            for pr in range(2, NPAIR):
+                if max(2 * pr - 8, pr - 2) == t:
+                    z_transpose(pr)
             add_b1(t)
             aggregate_1(t - 3)
-            if t % 2 == 0:
-                z_copy(t // 2 + 3)
+            for pr in range(2, NPAIR):
+                if max(2 * pr - 6, pr - 1) == t:
+                    z_copy(pr)
             gelu(t - 1)
             stats_1(t - 2)
-            if t % 4 == 1:
+            if t == 2:
+                z_quantise(1)
+            if t % 4 == 1 and t > 1:
                 z_quantise((t + 3) // 4)
-            if t == 1:
+            if t == 2:
                 let_go(1)
                 group_w2(1)
+                nc.gpsimd.tensor_copy(out=g1c[:], in_=g1b[:].rearrange("p g t -> p (g t)"))
+                nc.gpsimd.tensor_copy(out=be1c[:], in_=be1b[:].rearrange("p g t -> p (g t)"))
+            if t == 12:
+                load_second_norm()
             if t == 4:
                 quantise_w2()
             if t == NT:

@@ -251,9 +251,9 @@ def tile_emaaggregator_pa_t_kernel(tc, z, W1, b1, g1, be1, W2, b2, g2, be2, out)
             if not okh(grp):
                 return
             q, t = divmod(blk, 4)
-            if t == 0:
+            if ("hT", grp, q) not in live:
                 live["hT", grp, q] = work.tile([P, 4, SIZES[grp] * P], BF16, name="hT", tag="wr", bufs=4)
-            if grp == 0 and q == 0:
+            if (grp == 0 and q == 0) or blk == 7:
                 nc.vector.tensor_scalar(
                     out=live["hT", grp, q][:, t, :],
                     in0=live["ht", grp, blk][:],
@@ -277,11 +277,29 @@ def tile_emaaggregator_pa_t_kernel(tc, z, W1, b1, g1, be1, W2, b2, g2, be2, out)
             hg = work.tile([P, SIZES[grp] * P, 4], BF16, name="hg", tag="wg", bufs=3, align_bytes=64)
             dst = hg[:].rearrange("p (c i) t -> p c t i", i=4)
             src = live["hT", grp, q][:].rearrange("p t (c i) -> p c t i", i=4)
-            if q == 0 or grp == 0:
+            if grp == 0:
                 nc.vector.tensor_copy(out=dst, in_=src)
+            elif q == 0:
+                nc.gpsimd.tensor_scalar(
+                    out=hg[:],
+                    in0=live["hT", grp, q][:].rearrange("p t n -> p n t"),
+                    scalar1=live["go2", grp][:, 0:1],
+                    scalar2=0.0,
+                    op0=ALU.mult,
+                    op1=ALU.add,
+                )
             else:
                 nc.scalar.copy(out=dst, in_=src)
             live["hg", grp, q] = hg
+
+        def let_go2(grp):
+            if not okh(grp):
+                return
+            go2 = stats.tile([P, 1], F32, name="go2", tag="go2")
+            nc.vector.tensor_scalar(
+                out=go2[:], in0=neg_half[:, 0:1], scalar1=0.0, scalar2=1.0, op0=ALU.mult, op1=ALU.add
+            )
+            live["go2", grp] = go2
 
         def h_quantise(grp, q):
             if not okh(grp):
@@ -511,13 +529,17 @@ def tile_emaaggregator_pa_t_kernel(tc, z, W1, b1, g1, be1, W2, b2, g2, be2, out)
             h_transpose(blk + 4)
         interleave(0, 0)
         for s in range(NH + 2):
+            if s > 0:
+                interleave(s, 0)
+            affine_1(s, 7)
             for i in range(size(s - 1)):
                 add_b2(s - 1, i)
-            for blk in range(4, 8):
+            for blk in range(4, 7):
                 affine_1(s, blk)
                 if blk == 4:
                     rstd_2(s - 2)
                 h_transpose(8 * s + blk + 4)
+            h_transpose(8 * s + 11)
             scale_shift(s - 2, 0)
             neg_mean_2(s - 1)
             scale_shift(s - 2, 1)
@@ -531,16 +553,18 @@ def tile_emaaggregator_pa_t_kernel(tc, z, W1, b1, g1, be1, W2, b2, g2, be2, out)
             for blk in range(4):
                 affine_1(s + 1, blk)
                 h_transpose(8 * (s + 1) + blk + 4)
-            h_quantise(s, 1)
-            for i in range(size(s)):
-                matmul_2(s, i)
             if s == 1:
                 for i in range(ON_GPSIMD, NT):
                     normalise(i)
-            for i in range(2, size(s - 2)):
-                scale_shift(s - 2, i)
-                if i % 2 == 1:
-                    store(s - 2, i // 2)
-            interleave(s + 1, 0)
+            if size(s - 2) <= 2:
+                let_go2(s + 1)
+            h_quantise(s, 1)
+            for i in range(size(s)):
+                matmul_2(s, i)
+            if size(s - 2) > 2:
+                scale_shift(s - 2, 2)
+                let_go2(s + 1)
+                scale_shift(s - 2, 3)
+                store(s - 2, 1)
             for i in range(size(s - 1)):
                 square_2(s - 1, i)

@@ -63,6 +63,11 @@ def tile_emaaggregator_pa_t_kernel(tc, z, W1, b1, g1, be1, W2, b2, g2, be2, out)
         nc.scalar.dma_start(out=b1row[0:1, :], in_=b1.rearrange("(o f) -> o f", o=1))
         ones = const.tile([P, P], BF16, name="ones")
         nc.vector.memset(ones[:], 1.0)
+        gbrow = work.tile([P, 2 * D], BF16, name="gbrow", tag="x", bufs=4)
+        nc.vector.memset(gbrow[:], 0.0)
+        nc.scalar.dma_start(out=gbrow[0:1, 0:D], in_=g2.rearrange("(o f) -> o f", o=1))
+        nc.scalar.dma_start(out=gbrow[0:1, D : 2 * D], in_=be2.rearrange("(o f) -> o f", o=1))
+        gb = psum.tile([P, 2 * D], BF16, name="gb", tag="gb", bufs=1)
 
         zs = {}
 
@@ -90,13 +95,9 @@ def tile_emaaggregator_pa_t_kernel(tc, z, W1, b1, g1, be1, W2, b2, g2, be2, out)
         be1b = const.tile([P, 2, 4], BF16, name="be1b")
         nc.sync.dma_start(out=be1b[:], in_=be1.rearrange("(g p t) -> p g t", g=2, t=4))
         b2bc = const.tile([P, D], BF16, name="b2bc")
-        g2bc = const.tile([P, D], BF16, name="g2bc")
-        be2bc = const.tile([P, D], BF16, name="be2bc")
 
         def load_second_norm():
             nc.sync.dma_start(out=b2bc[:], in_=b2.partition_broadcast(P))
-            nc.sync.dma_start(out=g2bc[:], in_=g2.partition_broadcast(P))
-            nc.sync.dma_start(out=be2bc[:], in_=be2.partition_broadcast(P))
 
         neg_half = const.tile([P, 8], F32, name="neg_half")
         nc.gpsimd.memset(neg_half[:], -0.5)
@@ -122,7 +123,7 @@ def tile_emaaggregator_pa_t_kernel(tc, z, W1, b1, g1, be1, W2, b2, g2, be2, out)
             if not 0 <= pr < NPAIR:
                 return
             grp, h = divmod(pr, 2)
-            zt = psum.tile([P, 2, 2, P], F32, name="zt", tag="pb", bufs=4)
+            zt = psum.tile([P, 2, 2, P], F32, name="zt", tag="pb", bufs=3)
             for jj in range(2):
                 words = zs[grp][:, 2 * h + jj, :].bitcast(F32)
                 for u in range(2):
@@ -253,7 +254,7 @@ def tile_emaaggregator_pa_t_kernel(tc, z, W1, b1, g1, be1, W2, b2, g2, be2, out)
             q, t = divmod(blk, 4)
             if ("hT", grp, q) not in live:
                 live["hT", grp, q] = work.tile([P, 4, SIZES[grp] * P], BF16, name="hT", tag="wr", bufs=4)
-            if (grp == 0 and q == 0) or blk == 7:
+            if grp == 0 and q == 0:
                 nc.vector.tensor_scalar(
                     out=live["hT", grp, q][:, t, :],
                     in0=live["ht", grp, blk][:],
@@ -277,9 +278,9 @@ def tile_emaaggregator_pa_t_kernel(tc, z, W1, b1, g1, be1, W2, b2, g2, be2, out)
             hg = work.tile([P, SIZES[grp] * P, 4], BF16, name="hg", tag="wg", bufs=3, align_bytes=64)
             dst = hg[:].rearrange("p (c i) t -> p c t i", i=4)
             src = live["hT", grp, q][:].rearrange("p t (c i) -> p c t i", i=4)
-            if grp == 0:
+            if grp == 0 or (grp == 1 and q == 0):
                 nc.vector.tensor_copy(out=dst, in_=src)
-            elif q == 0:
+            else:
                 nc.gpsimd.tensor_scalar(
                     out=hg[:],
                     in0=live["hT", grp, q][:].rearrange("p t n -> p n t"),
@@ -288,8 +289,6 @@ def tile_emaaggregator_pa_t_kernel(tc, z, W1, b1, g1, be1, W2, b2, g2, be2, out)
                     op0=ALU.mult,
                     op1=ALU.add,
                 )
-            else:
-                nc.scalar.copy(out=dst, in_=src)
             live["hg", grp, q] = hg
 
         def let_go2(grp):
@@ -315,7 +314,7 @@ def tile_emaaggregator_pa_t_kernel(tc, z, W1, b1, g1, be1, W2, b2, g2, be2, out)
             if not okh(grp):
                 return
             cols = slice(P * i, P * (i + 1))
-            o = psum.tile([P, D], F32, name="o", tag="pb", bufs=4)
+            o = psum.tile([P, D], F32, name="o", tag="pb", bufs=3)
             for q in range(2):
                 hc, hs = live["hq", grp, q]
                 nc.tensor.matmul_mx(
@@ -394,7 +393,7 @@ def tile_emaaggregator_pa_t_kernel(tc, z, W1, b1, g1, be1, W2, b2, g2, be2, out)
                 out=live["q", grp, i // 2][:, i % 2, :],
                 in0=live["y", grp, i // 2][:, i % 2, :],
                 scalar=live["nm2", grp][:, i : i + 1],
-                in1=g2bc[:],
+                in1=gb[:, 0:D],
                 op0=ALU.add,
                 op1=ALU.mult,
             )
@@ -408,7 +407,7 @@ def tile_emaaggregator_pa_t_kernel(tc, z, W1, b1, g1, be1, W2, b2, g2, be2, out)
                 out=live["ot", grp, i // 2][:, i % 2, :],
                 in0=live["q", grp, i // 2][:, i % 2, :],
                 scalar=live["rs2", grp][:, i : i + 1],
-                in1=be2bc[:],
+                in1=gb[:, D : 2 * D],
                 op0=ALU.mult,
                 op1=ALU.add,
             )
@@ -510,6 +509,11 @@ def tile_emaaggregator_pa_t_kernel(tc, z, W1, b1, g1, be1, W2, b2, g2, be2, out)
                 group_w2(1)
                 nc.gpsimd.tensor_copy(out=g1c[:], in_=g1b[:].rearrange("p g t -> p (g t)"))
                 nc.gpsimd.tensor_copy(out=be1c[:], in_=be1b[:].rearrange("p g t -> p (g t)"))
+            if t == 1:
+                for g in range(2):
+                    nc.tensor.matmul(
+                        out=gb[:, D * g : D * (g + 1)], lhsT=ones[:], rhs=gbrow[:, D * g : D * (g + 1)], start=True, stop=True
+                    )
             if t == 12:
                 load_second_norm()
             if t == 4:
@@ -528,43 +532,42 @@ def tile_emaaggregator_pa_t_kernel(tc, z, W1, b1, g1, be1, W2, b2, g2, be2, out)
             affine_1(0, blk)
             h_transpose(blk + 4)
         interleave(0, 0)
+        for blk in range(4, 8):
+            affine_1(0, blk)
+            h_transpose(blk + 4)
+        interleave(0, 1)
         for s in range(NH + 2):
-            if s > 0:
-                interleave(s, 0)
-            affine_1(s, 7)
-            for i in range(size(s - 1)):
-                add_b2(s - 1, i)
-            for blk in range(4, 7):
-                affine_1(s, blk)
-                if blk == 4:
-                    rstd_2(s - 2)
-                h_transpose(8 * s + blk + 4)
-            h_transpose(8 * s + 11)
-            scale_shift(s - 2, 0)
-            neg_mean_2(s - 1)
-            scale_shift(s - 2, 1)
-            store(s - 2, 0)
-            interleave(s, 1)
-            for i in range(size(s - 1) // 2):
-                centre_gain(s - 1, i)
             h_quantise(s, 0)
-            for i in range(size(s - 1) // 2, size(s - 1)):
-                centre_gain(s - 1, i)
-            for blk in range(4):
-                affine_1(s + 1, blk)
-                h_transpose(8 * (s + 1) + blk + 4)
+            neg_mean_2(s - 1)
+            h_quantise(s, 1)
             if s == 1:
                 for i in range(ON_GPSIMD, NT):
                     normalise(i)
-            if size(s - 2) <= 2:
+            if s > 0:
                 let_go2(s + 1)
-            h_quantise(s, 1)
-            for i in range(size(s)):
+            for blk in range(4):
+                affine_1(s + 1, blk)
+                if blk == 0:
+                    rstd_2(s - 2)
+                h_transpose(8 * (s + 1) + blk + 4)
+            interleave(s + 1, 0)
+            if s == 0:
+                let_go2(s + 1)
+            for i in range(min(size(s), 3)):
                 matmul_2(s, i)
-            if size(s - 2) > 2:
-                scale_shift(s - 2, 2)
-                let_go2(s + 1)
-                scale_shift(s - 2, 3)
-                store(s - 2, 1)
+            for blk in range(4, 8):
+                affine_1(s + 1, blk)
+                h_transpose(8 * (s + 1) + blk + 4)
+            interleave(s + 1, 1)
+            for i in range(size(s - 1)):
+                centre_gain(s - 1, i)
+            for i in range(size(s - 2)):
+                scale_shift(s - 2, i)
+                if i % 2 == 1:
+                    store(s - 2, i // 2)
+            for i in range(size(s)):
+                add_b2(s, i)
+                if i == 0 and size(s) > 3:
+                    matmul_2(s, 3)
             for i in range(size(s - 1)):
                 square_2(s - 1, i)

@@ -21,7 +21,8 @@ GT = 4
 NG = NT // GT
 NPAIR = NT // 2
 BATCHES = [(4 * b, 4) for b in range(8)]
-ON_GPSIMD = 28
+LATE = 28
+LATE_SQUARES = {0: [28, 29, 30], 1: [31]}
 SIZES = [4, 4, 4, 4, 4, 4, 4, 2, 2]
 STARTS = [sum(SIZES[:g]) for g in range(len(SIZES))]
 NH = len(SIZES)
@@ -177,7 +178,7 @@ def tile_emaaggregator_pa_t_kernel(tc, z, W1, b1, g1, be1, W2, b2, g2, be2, out)
             first, j, count = batch_of[i]
             if j == 0:
                 live["raw", first] = stats.tile([P, 8, 2], F32, name="raw", tag="raw")
-            if i % 2 == 1:
+            if i % 2 == 1 or i >= LATE:
                 nc.scalar.activation(
                     out=acts[i][:], in_=live["x", i][:], func=ACT.Gelu, accum_out=live["raw", first][:, j, 0:1]
                 )
@@ -189,7 +190,7 @@ def tile_emaaggregator_pa_t_kernel(tc, z, W1, b1, g1, be1, W2, b2, g2, be2, out)
                 return
             first, j, count = batch_of[i]
             raw = live["raw", first]
-            if i % 2 == 1:
+            if i % 2 == 1 or i >= LATE:
                 junk = work.tile([P, F], BF16, name="junk", tag="junk", bufs=1)
                 nc.scalar.activation(
                     out=junk[:],
@@ -206,7 +207,7 @@ def tile_emaaggregator_pa_t_kernel(tc, z, W1, b1, g1, be1, W2, b2, g2, be2, out)
                 live["bs", i] = bs
 
         def aggregate_1(i):
-            if not tile_ok(i) or i % 2 == 1:
+            if not tile_ok(i) or i % 2 == 1 or i >= LATE:
                 return
             first, j, count = batch_of[i]
             nc.vector.bn_aggr(out=live["raw", first][:, j, :], in_=live["bs", i][:].rearrange("p c s -> p (c s)"))
@@ -225,10 +226,36 @@ def tile_emaaggregator_pa_t_kernel(tc, z, W1, b1, g1, be1, W2, b2, g2, be2, out)
             live["mv", first] = mv
             live["rs", first] = rs
 
+        def rstd_late(grp):
+            raw = live["raw", LATE]
+            nm = stats.tile([P, 4], F32, name="nm", tag="nm")
+            nc.gpsimd.tensor_scalar(
+                out=nm[:], in0=raw[:, 0:4, 0], scalar1=live["go2", grp][:, 0:1], scalar2=-1.0 / F, op0=ALU.mult, op1=ALU.mult
+            )
+            ve = stats.tile([P, 8], F32, name="ve", tag="ve")
+            nc.gpsimd.tensor_scalar(
+                out=ve[:, 0:4], in0=raw[:, 0:4, 1], scalar1=1.0 / F**3, scalar2=EPS, op0=ALU.mult, op1=ALU.add
+            )
+            rs = stats.tile([P, 8], F32, name="rs", tag="rs")
+            nc.gpsimd.tensor_tensor(out=rs[:, 0:4], in0=ve[:, 0:4], in1=neg_half[:, 0:4], op=ALU.pow)
+            nr = stats.tile([P, 4], F32, name="nr", tag="nr")
+            nc.gpsimd.tensor_tensor(out=nr[:], in0=nm[:], in1=rs[:, 0:4], op=ALU.mult)
+            live["rs", LATE] = rs
+            live["nr", LATE] = nr
+
+        def normalise_late(i):
+            j = i - LATE
+            nc.scalar.activation(
+                out=acts[i][:],
+                in_=acts[i][:],
+                func=ACT.Identity,
+                scale=live["rs", LATE][:, j : j + 1],
+                bias=live["nr", LATE][:, j : j + 1],
+            )
+
         def normalise(i):
             first, j, count = batch_of[i]
-            engine = nc.gpsimd if i < ON_GPSIMD else nc.vector
-            engine.tensor_scalar(
+            nc.gpsimd.tensor_scalar(
                 out=acts[i][:],
                 in0=acts[i][:],
                 scalar1=live["mv", first][:, j, 0:1],
@@ -486,7 +513,7 @@ def tile_emaaggregator_pa_t_kernel(tc, z, W1, b1, g1, be1, W2, b2, g2, be2, out)
         batch_end = {}
         for first, count in BATCHES:
             batch_end[first + count - 1] = (first, count)
-        for t in range(NT + 3):
+        for t in range(NT + 1):
             for grp in late_loads.get(t, []):
                 load_z(grp)
             matmul_1(t + 1)
@@ -499,7 +526,8 @@ def tile_emaaggregator_pa_t_kernel(tc, z, W1, b1, g1, be1, W2, b2, g2, be2, out)
                 if max(2 * pr - 6, pr - 1) == t:
                     z_copy(pr)
             gelu(t - 1)
-            stats_1(t - 2)
+            if t - 2 < LATE:
+                stats_1(t - 2)
             if t == 2:
                 z_quantise(1)
             if t % 4 == 1 and t > 1:
@@ -521,12 +549,11 @@ def tile_emaaggregator_pa_t_kernel(tc, z, W1, b1, g1, be1, W2, b2, g2, be2, out)
             if t == NT:
                 for n in range(4):
                     h_transpose(n)
-            if t - 2 in batch_end:
+            if t - 2 in batch_end and t - 2 < LATE:
                 first, count = batch_end[t - 2]
                 rstd_1(first, count)
                 for j in range(count):
-                    if first + j < ON_GPSIMD:
-                        normalise(first + j)
+                    normalise(first + j)
 
         for blk in range(4):
             affine_1(0, blk)
@@ -540,11 +567,10 @@ def tile_emaaggregator_pa_t_kernel(tc, z, W1, b1, g1, be1, W2, b2, g2, be2, out)
             h_quantise(s, 0)
             neg_mean_2(s - 1)
             h_quantise(s, 1)
-            if s == 1:
-                for i in range(ON_GPSIMD, NT):
-                    normalise(i)
             if s > 0:
                 let_go2(s + 1)
+            if s == 2:
+                rstd_late(s + 1)
             for blk in range(4):
                 affine_1(s + 1, blk)
                 if blk == 0:
@@ -571,3 +597,7 @@ def tile_emaaggregator_pa_t_kernel(tc, z, W1, b1, g1, be1, W2, b2, g2, be2, out)
                     matmul_2(s, 3)
             for i in range(size(s - 1)):
                 square_2(s - 1, i)
+            for i in LATE_SQUARES.get(s, []):
+                stats_1(i)
+            if 2 <= s < 6:
+                normalise_late(LATE + s - 2)

@@ -191,7 +191,7 @@ def tile_emaaggregator_pa_t_kernel(tc, z, W1, b1, g1, be1, W2, b2, g2, be2, out)
             first, j, count = batch_of[i]
             raw = live["raw", first]
             if i % 2 == 1 or i >= LATE:
-                junk = work.tile([P, F], BF16, name="junk", tag="junk", bufs=1)
+                junk = work.tile([P, F], BF16, name="junk", tag="junk", bufs=2)
                 nc.scalar.activation(
                     out=junk[:],
                     in_=acts[i][:],
@@ -377,7 +377,7 @@ def tile_emaaggregator_pa_t_kernel(tc, z, W1, b1, g1, be1, W2, b2, g2, be2, out)
                 return
             if i == 0:
                 live["sq2", grp] = stats.tile([P, GT], F32, name="sq2", tag="sq2")
-            junk2 = work.tile([P, D], BF16, name="junk2", tag="junk", bufs=1)
+            junk2 = work.tile([P, D], BF16, name="junk2", tag="junk", bufs=2)
             nc.scalar.activation(
                 out=junk2[:],
                 in_=live["y", grp, i // 2][:, i % 2, :],
@@ -587,14 +587,19 @@ def tile_emaaggregator_pa_t_kernel(tc, z, W1, b1, g1, be1, W2, b2, g2, be2, out)
             interleave(s + 1, 1)
             for i in range(size(s - 1)):
                 centre_gain(s - 1, i)
-            for i in range(size(s - 2)):
+            for i in range(min(size(s - 2), 2)):
                 scale_shift(s - 2, i)
-                if i % 2 == 1:
-                    store(s - 2, i // 2)
-            for i in range(size(s)):
+            store(s - 2, 0)
+            for i in range(min(size(s), 3)):
                 add_b2(s, i)
                 if i == 0 and size(s) > 3:
                     matmul_2(s, 3)
+            for i in range(2, size(s - 2)):
+                scale_shift(s - 2, i)
+            if size(s - 2) > 2:
+                store(s - 2, 1)
+            if size(s) > 3:
+                add_b2(s, 3)
             for i in range(size(s - 1)):
                 square_2(s - 1, i)
             for i in LATE_SQUARES.get(s, []):

@@ -305,7 +305,7 @@ def tile_emaaggregator_pa_t_kernel(tc, z, W1, b1, g1, be1, W2, b2, g2, be2, out)
             hg = work.tile([P, SIZES[grp] * P, 4], BF16, name="hg", tag="wg", bufs=3, align_bytes=64)
             dst = hg[:].rearrange("p (c i) t -> p c t i", i=4)
             src = live["hT", grp, q][:].rearrange("p t (c i) -> p c t i", i=4)
-            if grp == 0 or (grp == 1 and q == 0):
+            if grp <= 1:
                 nc.vector.tensor_copy(out=dst, in_=src)
             else:
                 nc.gpsimd.tensor_scalar(
@@ -443,7 +443,12 @@ def tile_emaaggregator_pa_t_kernel(tc, z, W1, b1, g1, be1, W2, b2, g2, be2, out)
             if not okh(grp):
                 return
             first = STARTS[grp] + 2 * half
+            if grp == NH - 1:
+                return
             nc.sync.dma_start(out=out_view[:, first : first + 2, :], in_=live["ot", grp, half][:])
+
+        def store_one(grp, i):
+            nc.sync.dma_start(out=out_view[:, STARTS[grp] + i, :], in_=live["ot", grp, i // 2][:, i % 2, :])
 
         z_transpose(0)
         w1g = []
@@ -577,8 +582,6 @@ def tile_emaaggregator_pa_t_kernel(tc, z, W1, b1, g1, be1, W2, b2, g2, be2, out)
                     rstd_2(s - 2)
                 h_transpose(8 * (s + 1) + blk + 4)
             interleave(s + 1, 0)
-            if s == 0:
-                let_go2(s + 1)
             for i in range(min(size(s), 3)):
                 matmul_2(s, i)
             for blk in range(4, 8):
@@ -589,6 +592,8 @@ def tile_emaaggregator_pa_t_kernel(tc, z, W1, b1, g1, be1, W2, b2, g2, be2, out)
                 centre_gain(s - 1, i)
             for i in range(min(size(s - 2), 2)):
                 scale_shift(s - 2, i)
+                if s - 2 == NH - 1:
+                    store_one(s - 2, i)
             store(s - 2, 0)
             for i in range(min(size(s), 3)):
                 add_b2(s, i)

@@ -22,8 +22,11 @@ NG = NT // GT
 NPAIR = NT // 2
 BATCHES = [(4 * b, 4) for b in range(8)]
 LATE = 28
-LATE_SQUARES = {0: [28, 29, 30], 1: [31]}
-SIZES = [4, 4, 4, 4, 4, 4, 4, 2, 2]
+LATE_SQUARES = {0: [28], 1: [29], 2: [30], 3: [31]}
+LATE_NORMALISE = {7: 28, 8: 29, 12: 30, 16: 31}
+SIZES = [4, 4, 4, 4, 4, 4, 4, 4]
+V_BANKS = [0, 1, 2, 3, 15, 17, 19, 23, 25, 27]
+WARM = False
 STARTS = [sum(SIZES[:g]) for g in range(len(SIZES))]
 NH = len(SIZES)
 
@@ -264,11 +267,13 @@ def tile_emaaggregator_pa_t_kernel(tc, z, W1, b1, g1, be1, W2, b2, g2, be2, out)
                 op1=ALU.mult,
             )
 
-        def h_transpose(n):
+        def h_transpose(n, warm=False):
             grp, blk = divmod(n, 8)
             if not okh(grp):
                 return
             ht = psum.tile([P, SIZES[grp] * P], F32, name="ht", tag="pa", bufs=4)
+            if warm:
+                nc.tensor.matmul(out=ht[:], lhsT=ones[:], rhs=b1p[:, 0:512], start=True, stop=True)
             for i in range(SIZES[grp]):
                 nc.tensor.transpose(
                     ht[:, P * i : P * (i + 1)], acts[STARTS[grp] + i][:, P * blk : P * (blk + 1)], ident[:]
@@ -281,7 +286,7 @@ def tile_emaaggregator_pa_t_kernel(tc, z, W1, b1, g1, be1, W2, b2, g2, be2, out)
             q, t = divmod(blk, 4)
             if ("hT", grp, q) not in live:
                 live["hT", grp, q] = work.tile([P, 4, SIZES[grp] * P], BF16, name="hT", tag="wr", bufs=4)
-            if grp == 0 and q == 0:
+            if 8 * grp + blk in V_BANKS:
                 nc.vector.tensor_scalar(
                     out=live["hT", grp, q][:, t, :],
                     in0=live["ht", grp, blk][:],
@@ -443,8 +448,6 @@ def tile_emaaggregator_pa_t_kernel(tc, z, W1, b1, g1, be1, W2, b2, g2, be2, out)
             if not okh(grp):
                 return
             first = STARTS[grp] + 2 * half
-            if grp == NH - 1:
-                return
             nc.sync.dma_start(out=out_view[:, first : first + 2, :], in_=live["ot", grp, half][:])
 
         def store_one(grp, i):
@@ -560,54 +563,57 @@ def tile_emaaggregator_pa_t_kernel(tc, z, W1, b1, g1, be1, W2, b2, g2, be2, out)
                 for j in range(count):
                     normalise(first + j)
 
-        for blk in range(4):
-            affine_1(0, blk)
-            h_transpose(blk + 4)
+        def evac(b):
+            affine_1(b // 8, b % 8)
+
+        def tile_of(n):
+            return divmod(n, 4) if 0 <= n < NT else (-1, 0)
+
+        for b in range(4):
+            evac(b)
+            h_transpose(b + 4)
         interleave(0, 0)
-        for blk in range(4, 8):
-            affine_1(0, blk)
-            h_transpose(blk + 4)
+        for b in range(4, 8):
+            evac(b)
+            h_transpose(b + 4)
         interleave(0, 1)
-        for s in range(NH + 2):
-            h_quantise(s, 0)
-            neg_mean_2(s - 1)
-            h_quantise(s, 1)
-            if s > 0:
-                let_go2(s + 1)
-            if s == 2:
-                rstd_late(s + 1)
-            for blk in range(4):
-                affine_1(s + 1, blk)
-                if blk == 0:
-                    rstd_2(s - 2)
-                h_transpose(8 * (s + 1) + blk + 4)
-            interleave(s + 1, 0)
-            for i in range(min(size(s), 3)):
-                matmul_2(s, i)
-            for blk in range(4, 8):
-                affine_1(s + 1, blk)
-                h_transpose(8 * (s + 1) + blk + 4)
-            interleave(s + 1, 1)
-            for i in range(size(s - 1)):
-                centre_gain(s - 1, i)
-            for i in range(min(size(s - 2), 2)):
-                scale_shift(s - 2, i)
-                if s - 2 == NH - 1:
-                    store_one(s - 2, i)
-            store(s - 2, 0)
-            for i in range(min(size(s), 3)):
-                add_b2(s, i)
-                if i == 0 and size(s) > 3:
-                    matmul_2(s, 3)
-            for i in range(2, size(s - 2)):
-                scale_shift(s - 2, i)
-            if size(s - 2) > 2:
-                store(s - 2, 1)
-            if size(s) > 3:
-                add_b2(s, 3)
-            for i in range(size(s - 1)):
-                square_2(s - 1, i)
-            for i in LATE_SQUARES.get(s, []):
-                stats_1(i)
-            if 2 <= s < 6:
-                normalise_late(LATE + s - 2)
+        for b in range(8, 12):
+            evac(b)
+            if b < 10:
+                h_transpose(b + 4)
+        for tau in range(NT + 9):
+            g, i = divmod(tau, 4)
+            if i == 0:
+                add_b2(*tile_of(tau - 1))
+                h_quantise(g, 0)
+                neg_mean_2(g - 1)
+                h_quantise(g, 1)
+                let_go2(g + 1)
+            h_transpose(2 * tau + 14, WARM)
+            h_transpose(2 * tau + 15)
+            if tau < NT:
+                matmul_2(g, i)
+            if i == 0:
+                interleave(g + 1, 0)
+            if i == 2:
+                interleave(g + 1, 1)
+            evac(2 * tau + 12)
+            if i == 2:
+                rstd_2(g - 1)
+            evac(2 * tau + 13)
+            if 0 <= tau - 8 < NT:
+                scale_shift(*tile_of(tau - 8))
+                if tau - 8 >= NT - 2:
+                    store_one(*tile_of(tau - 8))
+                elif tau % 2 == 1:
+                    store((tau - 8) // 4, ((tau - 8) % 4) // 2)
+            centre_gain(*tile_of(tau - 4))
+            if i != 0:
+                add_b2(*tile_of(tau - 1))
+            square_2(*tile_of(tau - 2))
+            for n in LATE_SQUARES.get(tau, []):
+                stats_1(n)
+            if tau == 3:
+                rstd_late(1)
+            if tau in LATE_NORMALISE:
+                normalise_late(LATE_NORMALISE[tau])

@@ -25,8 +25,9 @@ LATE = 28
 LATE_SQUARES = {0: [28], 1: [29], 2: [30], 3: [31]}
 LATE_NORMALISE = {7: 28, 8: 29, 12: 30, 16: 31}
 SIZES = [4, 4, 4, 4, 4, 4, 4, 4]
-V_BANKS = [0, 1, 2, 3, 15, 17, 19, 23, 25, 27]
+V_BANKS = [0, 1, 2, 3, 4, 5, 15, 17, 19, 23, 25, 27]
 WARM = False
+G_TILES = {22: (28, 31), 23: (28, 33), 24: (30, 35), 25: (30, 37)}
 STARTS = [sum(SIZES[:g]) for g in range(len(SIZES))]
 NH = len(SIZES)
 
@@ -444,6 +445,29 @@ def tile_emaaggregator_pa_t_kernel(tc, z, W1, b1, g1, be1, W2, b2, g2, be2, out)
                 op1=ALU.add,
             )
 
+        def finish_on_gpsimd(grp, i):
+            if i % 2 == 0:
+                live["q", grp, i // 2] = work.tile([P, 2, D], F32, name="q", tag="x", bufs=4)
+                live["ot", grp, i // 2] = work.tile([P, 2, D], F32, name="ot", tag="wr", bufs=4)
+            q = live["q", grp, i // 2][:, i % 2, :]
+            if ("nr2", grp) not in live:
+                live["nr2", grp] = stats.tile([P, GT], F32, name="nr2", tag="nr2")
+            nc.scalar.activation(
+                out=live["nr2", grp][:, i : i + 1],
+                in_=live["nm2", grp][:, i : i + 1],
+                func=ACT.Identity,
+                scale=live["rs2", grp][:, i : i + 1],
+            )
+            nc.scalar.activation(
+                out=q,
+                in_=live["y", grp, i // 2][:, i % 2, :],
+                func=ACT.Identity,
+                scale=live["rs2", grp][:, i : i + 1],
+                bias=live["nr2", grp][:, i : i + 1],
+            )
+            nc.gpsimd.tensor_tensor(out=q, in0=q, in1=gbs[:, 0:D], op=ALU.mult)
+            nc.gpsimd.tensor_tensor(out=live["ot", grp, i // 2][:, i % 2, :], in0=q, in1=gbs[:, D : 2 * D], op=ALU.add)
+
         def store(grp, half):
             if not okh(grp):
                 return
@@ -569,6 +593,7 @@ def tile_emaaggregator_pa_t_kernel(tc, z, W1, b1, g1, be1, W2, b2, g2, be2, out)
         def tile_of(n):
             return divmod(n, 4) if 0 <= n < NT else (-1, 0)
 
+        gbs = const.tile([P, 2 * D], BF16, name="gbs")
         for b in range(4):
             evac(b)
             h_transpose(b + 4)
@@ -601,13 +626,21 @@ def tile_emaaggregator_pa_t_kernel(tc, z, W1, b1, g1, be1, W2, b2, g2, be2, out)
             if i == 2:
                 rstd_2(g - 1)
             evac(2 * tau + 13)
-            if 0 <= tau - 8 < NT:
+            if tau == 8:
+                nc.scalar.copy(out=gbs[:], in_=gb[:])
+            if 0 <= tau - 8 < NT and tau - 8 not in G_TILES:
                 scale_shift(*tile_of(tau - 8))
                 if tau - 8 >= NT - 2:
                     store_one(*tile_of(tau - 8))
                 elif tau % 2 == 1:
                     store((tau - 8) // 4, ((tau - 8) % 4) // 2)
-            centre_gain(*tile_of(tau - 4))
+            if tau - 4 not in G_TILES:
+                centre_gain(*tile_of(tau - 4))
+            for n in G_TILES:
+                if G_TILES[n][0] == tau:
+                    finish_on_gpsimd(*tile_of(n))
+                if G_TILES[n][1] == tau:
+                    store_one(*tile_of(n))
             if i != 0:
                 add_b2(*tile_of(tau - 1))
             square_2(*tile_of(tau - 2))

@@ -25,7 +25,7 @@ LATE = 28
 LATE_SQUARES = {0: [28], 1: [29], 2: [30], 3: [31]}
 LATE_NORMALISE = {7: 28, 8: 29, 12: 30, 16: 31}
 SIZES = [4, 4, 4, 4, 4, 4, 4, 4]
-V_BANKS = [0, 1, 2, 3, 4, 5, 15, 17, 19, 23, 25, 27]
+V_BANKS = [0, 1, 2, 3, 4, 5] + list(range(9, 28, 2))
 WARM = False
 G_TILES = {22: (28, 31), 23: (28, 33), 24: (30, 35), 25: (30, 37)}
 STARTS = [sum(SIZES[:g]) for g in range(len(SIZES))]
@@ -311,7 +311,7 @@ def tile_emaaggregator_pa_t_kernel(tc, z, W1, b1, g1, be1, W2, b2, g2, be2, out)
             hg = work.tile([P, SIZES[grp] * P, 4], BF16, name="hg", tag="wg", bufs=3, align_bytes=64)
             dst = hg[:].rearrange("p (c i) t -> p c t i", i=4)
             src = live["hT", grp, q][:].rearrange("p t (c i) -> p c t i", i=4)
-            if grp <= 1:
+            if grp <= 0:
                 nc.vector.tensor_copy(out=dst, in_=src)
             else:
                 nc.gpsimd.tensor_scalar(

@@ -26,6 +26,8 @@ LATE_SQUARES = {0: [28], 1: [29], 2: [30], 3: [31]}
 LATE_NORMALISE = {7: 28, 8: 29, 12: 30, 16: 31}
 SIZES = [4, 4, 4, 4, 4, 4, 4, 4]
 V_BANKS = [0, 1, 2, 3, 4, 5] + list(range(9, 28, 2))
+V_STATS = [0, 4]
+V_ZCOPY = 4
 WARM = False
 G_TILES = {22: (28, 31), 23: (28, 33), 24: (30, 35), 25: (30, 37)}
 STARTS = [sum(SIZES[:g]) for g in range(len(SIZES))]
@@ -111,10 +113,11 @@ def tile_emaaggregator_pa_t_kernel(tc, z, W1, b1, g1, be1, W2, b2, g2, be2, out)
         ident = const.tile([P, P], F32, name="ident")
         make_identity(nc, ident[:])
         unit = const.tile([P, 8, 2], F32, name="unit")
-        nc.gpsimd.memset(unit[:, 0:8:2, 0:1], -1.0)
-        nc.gpsimd.memset(unit[:, 0:8:2, 1:2], 1.0)
-        nc.gpsimd.memset(unit[:, 1:8:2, 0:1], -1.0 / F)
-        nc.gpsimd.memset(unit[:, 1:8:2, 1:2], 1.0 / F**3)
+        nc.gpsimd.memset(unit[:, :, 0:1], -1.0 / F)
+        nc.gpsimd.memset(unit[:, :, 1:2], 1.0 / F**3)
+        for j in V_STATS:
+            nc.gpsimd.memset(unit[:, j, 0:1], -1.0)
+            nc.gpsimd.memset(unit[:, j, 1:2], 1.0)
         eps_col = const.tile([P, 1], F32, name="eps_col")
         nc.vector.tensor_scalar(
             out=eps_col[:], in0=neg_half[:, 0:1], scalar1=0.0, scalar2=EPS, op0=ALU.mult, op1=ALU.add
@@ -142,7 +145,10 @@ def tile_emaaggregator_pa_t_kernel(tc, z, W1, b1, g1, be1, W2, b2, g2, be2, out)
             if h == 0:
                 live["zg", grp] = work.tile([P, GT * P * 4], BF16, name="zg", tag="zg", bufs=4, align_bytes=64)
             zgw = live["zg", grp][:].bitcast(F32).rearrange("p (j r u) -> p j r u", j=GT, u=2)
-            nc.scalar.copy(out=zgw[:, 2 * h : 2 * h + 2, :, :], in_=live["zt", pr][:].rearrange("p j u r -> p j r u"))
+            if pr >= V_ZCOPY:
+                nc.vector.tensor_copy(out=zgw[:, 2 * h : 2 * h + 2, :, :], in_=live["zt", pr][:].rearrange("p j u r -> p j r u"))
+            else:
+                nc.scalar.copy(out=zgw[:, 2 * h : 2 * h + 2, :, :], in_=live["zt", pr][:].rearrange("p j u r -> p j r u"))
 
         def z_quantise(grp):
             if not ok(grp):
@@ -182,7 +188,7 @@ def tile_emaaggregator_pa_t_kernel(tc, z, W1, b1, g1, be1, W2, b2, g2, be2, out)
             first, j, count = batch_of[i]
             if j == 0:
                 live["raw", first] = stats.tile([P, 8, 2], F32, name="raw", tag="raw")
-            if i % 2 == 1 or i >= LATE:
+            if i % 8 not in V_STATS or i >= LATE:
                 nc.scalar.activation(
                     out=acts[i][:], in_=live["x", i][:], func=ACT.Gelu, accum_out=live["raw", first][:, j, 0:1]
                 )
@@ -194,7 +200,7 @@ def tile_emaaggregator_pa_t_kernel(tc, z, W1, b1, g1, be1, W2, b2, g2, be2, out)
                 return
             first, j, count = batch_of[i]
             raw = live["raw", first]
-            if i % 2 == 1 or i >= LATE:
+            if i % 8 not in V_STATS or i >= LATE:
                 junk = work.tile([P, F], BF16, name="junk", tag="junk", bufs=2)
                 nc.scalar.activation(
                     out=junk[:],
@@ -211,7 +217,7 @@ def tile_emaaggregator_pa_t_kernel(tc, z, W1, b1, g1, be1, W2, b2, g2, be2, out)
                 live["bs", i] = bs
 
         def aggregate_1(i):
-            if not tile_ok(i) or i % 2 == 1 or i >= LATE:
+            if not tile_ok(i) or i % 8 not in V_STATS or i >= LATE:
                 return
             first, j, count = batch_of[i]
             nc.vector.bn_aggr(out=live["raw", first][:, j, :], in_=live["bs", i][:].rearrange("p c s -> p (c s)"))
@@ -219,7 +225,7 @@ def tile_emaaggregator_pa_t_kernel(tc, z, W1, b1, g1, be1, W2, b2, g2, be2, out)
         def rstd_1(first, count):
             mv = stats.tile([P, 8, 2], F32, name="mv", tag="mv")
             nc.gpsimd.tensor_tensor(
-                out=mv[:, 0:count, :], in0=live["raw", first][:, 0:count, :], in1=unit[:, 0:count, :], op=ALU.mult
+                out=mv[:, 0:count, :], in0=live["raw", first][:, 0:count, :], in1=unit[:, first % 8 : first % 8 + count, :], op=ALU.mult
             )
             ve = stats.tile([P, 8], F32, name="ve", tag="ve")
             nc.gpsimd.tensor_scalar(

@@ -78,10 +78,15 @@ def tile_emaaggregator_pa_t_kernel(tc, z, W1, b1, g1, be1, W2, b2, g2, be2, out)
 
         zs = {}
 
-        def load_z(grp):
-            t = work.tile([P, GT, D], BF16, name="zs", tag="zs", bufs=4)
-            nc.sync.dma_start(out=t[:], in_=z_view[:, GT * grp : GT * (grp + 1), :])
-            zs[grp] = t
+        def load_z(grp, half=None):
+            if half in (None, 0):
+                zs[grp] = work.tile([P, GT, D], BF16, name="zs", tag="zs", bufs=4)
+            t = zs[grp]
+            if half is None:
+                nc.sync.dma_start(out=t[:], in_=z_view[:, GT * grp : GT * (grp + 1), :])
+            else:
+                first = GT * grp + 2 * half
+                nc.sync.dma_start(out=t[:, 2 * half : 2 * half + 2, :], in_=z_view[:, first : first + 2, :])
 
         w1raw = []
         w2raw = []
@@ -90,12 +95,13 @@ def tile_emaaggregator_pa_t_kernel(tc, z, W1, b1, g1, be1, W2, b2, g2, be2, out)
             t = work.tile([P, 4, 512], BF16, name="w1raw", tag="wr", bufs=4)
             nc.sync.dma_start(out=t[:], in_=w1_view[:, :, 512 * g : 512 * (g + 1)])
             w1raw.append(t)
-            load_z(g)
+            load_z(0, g)
+        load_z(1)
+        load_z(2)
         for g in range(2):
             t = work.tile([P, 4, 512], BF16, name="w2raw", tag="wr", bufs=4)
             nc.sync.dma_start(out=t[:], in_=W2[512 * g : 512 * (g + 1), :].rearrange("(p j) d -> p j d", j=4))
             w2raw.append(t)
-        load_z(2)
         load_z(3)
         g1b = const.tile([P, 2, 4], BF16, name="g1b")
         nc.sync.dma_start(out=g1b[:], in_=g1.rearrange("(g p t) -> p g t", g=2, t=4))
@@ -150,13 +156,21 @@ def tile_emaaggregator_pa_t_kernel(tc, z, W1, b1, g1, be1, W2, b2, g2, be2, out)
             else:
                 nc.scalar.copy(out=zgw[:, 2 * h : 2 * h + 2, :, :], in_=live["zt", pr][:].rearrange("p j u r -> p j r u"))
 
-        def z_quantise(grp):
+        def z_quantise(grp, half=None):
             if not ok(grp):
                 return
-            zc = work.tile([P, GT * P], U32, name="zc", tag="codes", bufs=4, align_bytes=64)
-            zsc = work.tile([P, GT * P], U8, name="zsc", tag="scales", bufs=4, align_bytes=64)
-            nc.vector.quantize_mx(out=zc[:].bitcast(FP8X4), scales=zsc[:], in_=live["zg", grp][:])
-            live["zq", grp] = (zc, zsc)
+            if half in (None, 0):
+                zc = work.tile([P, GT * P], U32, name="zc", tag="codes", bufs=4, align_bytes=64)
+                zsc = work.tile([P, GT * P], U8, name="zsc", tag="scales", bufs=4, align_bytes=64)
+                live["zq", grp] = (zc, zsc)
+            zc, zsc = live["zq", grp]
+            if half is None:
+                nc.vector.quantize_mx(out=zc[:].bitcast(FP8X4), scales=zsc[:], in_=live["zg", grp][:])
+            else:
+                c = slice(2 * P * half, 2 * P * (half + 1))
+                nc.vector.quantize_mx(
+                    out=zc[:, c].bitcast(FP8X4), scales=zsc[:, c], in_=live["zg", grp][:, 8 * P * half : 8 * P * (half + 1)]
+                )
 
         def matmul_1(i):
             if not tile_ok(i):
@@ -492,19 +506,20 @@ def tile_emaaggregator_pa_t_kernel(tc, z, W1, b1, g1, be1, W2, b2, g2, be2, out)
         w1c = const.tile([P, F], U32, name="w1c", align_bytes=64)
         w1s = const.tile([P, F], U8, name="w1s", align_bytes=64)
         nc.vector.tensor_copy(out=dst[0][:, 0:2], in_=src[0][:, 0:2])
-        nc.vector.tensor_copy(out=dst[0][:, 2:4], in_=src[0][:, 2:4])
-        nc.scalar.copy(out=dst[1][:, 2:4], in_=src[1][:, 2:4])
+        nc.scalar.copy(out=dst[0][:, 2:4], in_=src[0][:, 2:4])
         z_copy(0)
+        nc.vector.quantize_mx(out=w1c[:, 0:512].bitcast(FP8X4), scales=w1s[:, 0:512], in_=w1g[0][:])
         z_transpose(1)
         b1ps = []
         for g in range(2):
             b1ps.append(psum.tile([P, 512], F32, name="b1ps", tag="pa", bufs=4))
             nc.tensor.matmul(out=b1ps[g][:], lhsT=ones[:], rhs=b1row[:, 512 * g : 512 * (g + 1)], start=True, stop=True)
-        z_copy(1)
         nc.vector.tensor_copy(out=dst[1][:, 0:2], in_=src[1][:, 0:2])
-        nc.vector.quantize_mx(out=w1c[:, 0:512].bitcast(FP8X4), scales=w1s[:, 0:512], in_=w1g[0][:])
+        nc.scalar.copy(out=dst[1][:, 2:4], in_=src[1][:, 2:4])
+        z_quantise(0, 0)
+        z_copy(1)
         nc.vector.quantize_mx(out=w1c[:, 512:1024].bitcast(FP8X4), scales=w1s[:, 512:1024], in_=w1g[1][:])
-        z_quantise(0)
+        z_quantise(0, 1)
         go = [const.tile([P, 1], F32, name="go%d" % g) for g in range(2)]
 
         def let_go(g):

@@ -67,13 +67,10 @@ def tile_emaaggregator_pa_t_kernel(tc, z, W1, b1, g1, be1, W2, b2, g2, be2, out)
 
         b1row = work.tile([P, F], BF16, name="b1row", tag="x", bufs=4)
         nc.vector.memset(b1row[:], 0.0)
-        nc.scalar.dma_start(out=b1row[0:1, :], in_=b1.rearrange("(o f) -> o f", o=1))
         ones = const.tile([P, P], BF16, name="ones")
         nc.vector.memset(ones[:], 1.0)
         gbrow = work.tile([P, 2 * D], BF16, name="gbrow", tag="x", bufs=4)
         nc.vector.memset(gbrow[:], 0.0)
-        nc.scalar.dma_start(out=gbrow[0:1, 0:D], in_=g2.rearrange("(o f) -> o f", o=1))
-        nc.scalar.dma_start(out=gbrow[0:1, D : 2 * D], in_=be2.rearrange("(o f) -> o f", o=1))
         gb = psum.tile([P, 2 * D], BF16, name="gb", tag="gb", bufs=1)
 
         zs = {}
@@ -96,6 +93,10 @@ def tile_emaaggregator_pa_t_kernel(tc, z, W1, b1, g1, be1, W2, b2, g2, be2, out)
             nc.sync.dma_start(out=t[:], in_=w1_view[:, :, 512 * g : 512 * (g + 1)])
             w1raw.append(t)
             load_z(0, g)
+            if g == 0:
+                nc.sync.dma_start(out=b1row[0:1, :], in_=b1.rearrange("(o f) -> o f", o=1))
+        nc.sync.dma_start(out=gbrow[0:1, 0:D], in_=g2.rearrange("(o f) -> o f", o=1))
+        nc.sync.dma_start(out=gbrow[0:1, D : 2 * D], in_=be2.rearrange("(o f) -> o f", o=1))
         load_z(1)
         load_z(2)
         for g in range(2):

@@ -28,6 +28,9 @@ SIZES = [4, 4, 4, 4, 4, 4, 4, 4]
 V_BANKS = [0, 1, 2, 3, 4, 5] + list(range(9, 28, 2))
 V_STATS = [0, 4]
 V_ZCOPY = 4
+LAG = 7
+LAG_END = 6
+ONE_BY_ONE = NT - 6
 WARM = False
 G_TILES = {22: (28, 31), 23: (28, 33), 24: (30, 35), 25: (30, 37)}
 STARTS = [sum(SIZES[:g]) for g in range(len(SIZES))]
@@ -507,20 +510,25 @@ def tile_emaaggregator_pa_t_kernel(tc, z, W1, b1, g1, be1, W2, b2, g2, be2, out)
         w1c = const.tile([P, F], U32, name="w1c", align_bytes=64)
         w1s = const.tile([P, F], U8, name="w1s", align_bytes=64)
         nc.vector.tensor_copy(out=dst[0][:, 0:2], in_=src[0][:, 0:2])
-        nc.scalar.copy(out=dst[0][:, 2:4], in_=src[0][:, 2:4])
+        nc.vector.tensor_copy(out=dst[0][:, 2:4], in_=src[0][:, 2:4])
         z_copy(0)
         nc.vector.quantize_mx(out=w1c[:, 0:512].bitcast(FP8X4), scales=w1s[:, 0:512], in_=w1g[0][:])
-        z_transpose(1)
         b1ps = []
         for g in range(2):
             b1ps.append(psum.tile([P, 512], F32, name="b1ps", tag="pa", bufs=4))
             nc.tensor.matmul(out=b1ps[g][:], lhsT=ones[:], rhs=b1row[:, 512 * g : 512 * (g + 1)], start=True, stop=True)
+        z_transpose(1)
         nc.vector.tensor_copy(out=dst[1][:, 0:2], in_=src[1][:, 0:2])
         nc.scalar.copy(out=dst[1][:, 2:4], in_=src[1][:, 2:4])
         z_quantise(0, 0)
+        b1p = const.tile([P, F], BF16, name="b1p")
+        for g in range(2):
+            nc.scalar.copy(
+                out=b1p[:, 512 * g : 512 * (g + 1)].rearrange("p (t m) -> p t m", t=4),
+                in_=b1ps[g][:].rearrange("p (m t) -> p t m", t=4),
+            )
         z_copy(1)
         nc.vector.quantize_mx(out=w1c[:, 512:1024].bitcast(FP8X4), scales=w1s[:, 512:1024], in_=w1g[1][:])
-        z_quantise(0, 1)
         go = [const.tile([P, 1], F32, name="go%d" % g) for g in range(2)]
 
         def let_go(g):
@@ -528,13 +536,6 @@ def tile_emaaggregator_pa_t_kernel(tc, z, W1, b1, g1, be1, W2, b2, g2, be2, out)
                 out=go[g][:], in0=neg_half[:, 0:1], scalar1=0.0, scalar2=1.0, op0=ALU.mult, op1=ALU.add
             )
 
-        let_go(0)
-        b1p = const.tile([P, F], BF16, name="b1p")
-        for g in range(2):
-            nc.scalar.copy(
-                out=b1p[:, 512 * g : 512 * (g + 1)].rearrange("p (t m) -> p t m", t=4),
-                in_=b1ps[g][:].rearrange("p (m t) -> p t m", t=4),
-            )
         g1c = const.tile([P, 8], F32, name="g1c")
         be1c = const.tile([P, 8], F32, name="be1c")
         matmul_1(0)
@@ -553,7 +554,6 @@ def tile_emaaggregator_pa_t_kernel(tc, z, W1, b1, g1, be1, W2, b2, g2, be2, out)
                 op1=ALU.add,
             )
 
-        group_w2(0)
 
         def quantise_w2():
             for g in range(2):
@@ -575,6 +575,10 @@ def tile_emaaggregator_pa_t_kernel(tc, z, W1, b1, g1, be1, W2, b2, g2, be2, out)
                 if max(2 * pr - 8, pr - 2) == t:
                     z_transpose(pr)
             add_b1(t)
+            if t == 0:
+                z_quantise(0, 1)
+                let_go(0)
+                group_w2(0)
             aggregate_1(t - 3)
             for pr in range(2, NPAIR):
                 if max(2 * pr - 6, pr - 1) == t:
@@ -645,17 +649,21 @@ def tile_emaaggregator_pa_t_kernel(tc, z, W1, b1, g1, be1, W2, b2, g2, be2, out)
             if i == 2:
                 interleave(g + 1, 1)
             evac(2 * tau + 12)
-            if i == 2:
+            if i == 2 and g < NH:
                 rstd_2(g - 1)
+            if tau == NT + 1:
+                square_2(*tile_of(NT - 1))
+                rstd_2(NH - 1)
             evac(2 * tau + 13)
             if tau == 8:
                 nc.scalar.copy(out=gbs[:], in_=gb[:])
-            if 0 <= tau - 8 < NT and tau - 8 not in G_TILES:
-                scale_shift(*tile_of(tau - 8))
-                if tau - 8 >= NT - 2:
-                    store_one(*tile_of(tau - 8))
-                elif tau % 2 == 1:
-                    store((tau - 8) // 4, ((tau - 8) % 4) // 2)
+            for n in range(NT):
+                if n + (LAG if n < NT - 4 else LAG_END) == tau and n not in G_TILES:
+                    scale_shift(*tile_of(n))
+                    if n >= ONE_BY_ONE:
+                        store_one(*tile_of(n))
+                    elif n % 2 == 1:
+                        store(n // 4, (n % 4) // 2)
             if tau - 4 not in G_TILES:
                 centre_gain(*tile_of(tau - 4))
             for n in G_TILES:
@@ -665,7 +673,8 @@ def tile_emaaggregator_pa_t_kernel(tc, z, W1, b1, g1, be1, W2, b2, g2, be2, out)
                     store_one(*tile_of(n))
             if i != 0:
                 add_b2(*tile_of(tau - 1))
-            square_2(*tile_of(tau - 2))
+            if tau != NT + 1:
+                square_2(*tile_of(tau - 2))
             for n in LATE_SQUARES.get(tau, []):
                 stats_1(n)
             if tau == 3:

@@ -32,7 +32,9 @@ LAG = 7
 LAG_END = 6
 ONE_BY_ONE = NT - 6
 WARM = False
-G_TILES = {22: (28, 31), 23: (28, 33), 24: (30, 35), 25: (30, 37)}
+G_TILES = {22: (26, 29), 23: (26, 30), 24: (28, 32), 25: (28, 34)}
+EARLY_RSTD = 6
+S_INTERLEAVE = (7, 1)
 STARTS = [sum(SIZES[:g]) for g in range(len(SIZES))]
 NH = len(SIZES)
 
@@ -337,6 +339,8 @@ def tile_emaaggregator_pa_t_kernel(tc, z, W1, b1, g1, be1, W2, b2, g2, be2, out)
             src = live["hT", grp, q][:].rearrange("p t (c i) -> p c t i", i=4)
             if grp <= 0:
                 nc.vector.tensor_copy(out=dst, in_=src)
+            elif (grp, q) == S_INTERLEAVE:
+                nc.scalar.copy(out=hg[:], in_=live["hT", grp, q][:].rearrange("p t n -> p n t"))
             else:
                 nc.gpsimd.tensor_scalar(
                     out=hg[:],
@@ -427,19 +431,18 @@ def tile_emaaggregator_pa_t_kernel(tc, z, W1, b1, g1, be1, W2, b2, g2, be2, out)
             )
             live["nm2", grp] = nm2
 
-        def rstd_2(grp):
+        def rstd_2(grp, first=0, n=GT):
             if not okh(grp):
                 return
-            rs2 = stats.tile([P, GT], F32, name="rs2", tag="rs2")
-            n = SIZES[grp]
+            if ("rs2", grp) not in live:
+                live["rs2", grp] = stats.tile([P, GT], F32, name="rs2", tag="rs2")
             nc.scalar.activation(
-                out=rs2[:, 0:n],
-                in_=live["sq2", grp][:, 0:n],
+                out=live["rs2", grp][:, first:n],
+                in_=live["sq2", grp][:, first:n],
                 func=ACT.Abs_reciprocal_sqrt,
                 scale=1.0 / D**3,
                 bias=eps_col[:, 0:1],
             )
-            live["rs2", grp] = rs2
 
         def centre_gain(grp, i):
             if not okh(grp):
@@ -646,11 +649,13 @@ def tile_emaaggregator_pa_t_kernel(tc, z, W1, b1, g1, be1, W2, b2, g2, be2, out)
                 matmul_2(g, i)
             if i == 0:
                 interleave(g + 1, 0)
-            if i == 2:
+            if i == 2 and (g + 1, 1) != S_INTERLEAVE:
                 interleave(g + 1, 1)
             evac(2 * tau + 12)
             if i == 2 and g < NH:
-                rstd_2(g - 1)
+                rstd_2(g - 1, 2 if g - 1 == EARLY_RSTD else 0)
+            if i == 0 and g - 1 == EARLY_RSTD:
+                rstd_2(g - 1, 0, 2)
             if tau == NT + 1:
                 square_2(*tile_of(NT - 1))
                 rstd_2(NH - 1)
@@ -669,6 +674,8 @@ def tile_emaaggregator_pa_t_kernel(tc, z, W1, b1, g1, be1, W2, b2, g2, be2, out)
             for n in G_TILES:
                 if G_TILES[n][0] == tau:
                     finish_on_gpsimd(*tile_of(n))
+                    if n == 22:
+                        interleave(*S_INTERLEAVE)
                 if G_TILES[n][1] == tau:
                     store_one(*tile_of(n))
             if i != 0:

from contextlib import ExitStack

import concourse.mybir as mybir
from concourse.masks import make_identity

B, D, F = 4096, 512, 1024
EPS = 1e-5
FLOPS = 2 * B * D * F * 2

F32 = mybir.dt.float32
BF16 = mybir.dt.bfloat16
U32 = mybir.dt.uint32
U8 = mybir.dt.uint8
FP8X4 = mybir.dt.float8_e4m3fn_x4
ALU = mybir.AluOpType
ACT = mybir.ActivationFunctionType

P = 128
NT = B // P
GT = 4
NG = NT // GT
NPAIR = NT // 2
BATCHES = [(4 * b, 4) for b in range(8)]
LATE = 28
LATE_SQUARES = {0: [28], 1: [29], 2: [30], 3: [31]}
LATE_NORMALISE = {7: 28, 8: 29, 12: 30, 16: 31}
SIZES = [4, 4, 4, 4, 4, 4, 4, 4]
V_BANKS = [0, 1, 2, 3, 4, 5] + list(range(9, 28, 2))
V_STATS = [0, 4]
V_ZCOPY = 4
LAG = 7
LAG_END = 6
ONE_BY_ONE = NT - 6
WARM = False
G_TILES = {22: (26, 29), 23: (26, 30), 24: (28, 32), 25: (28, 34)}
EARLY_RSTD = 6
S_INTERLEAVE = (7, 1)
STARTS = [sum(SIZES[:g]) for g in range(len(SIZES))]
NH = len(SIZES)


def tile_emaaggregator_pa_t_kernel(tc, z, W1, b1, g1, be1, W2, b2, g2, be2, out):
    nc = tc.nc
    z_view = z.rearrange("(p i) k -> p i k", i=NT)
    out_view = out.rearrange("(p i) d -> p i d", i=NT)

    with ExitStack() as ctx:
        const = ctx.enter_context(tc.tile_pool(name="const", bufs=1))
        work = ctx.enter_context(tc.tile_pool(name="work", bufs=2))
        stats = ctx.enter_context(tc.tile_pool(name="stats", bufs=3))
        psum = ctx.enter_context(tc.psum_pool(name="psum", bufs=2))
        ctx.enter_context(tc.manual_schedule())

        live = {}

        def ok(grp):
            return 0 <= grp < NG

        def tile_ok(i):
            return 0 <= i < NT

        def okh(grp):
            return 0 <= grp < NH

        def size(grp):
            return SIZES[grp] if okh(grp) else 0

        batch_of = {}
        for first, count in BATCHES:
            for j in range(count):
                batch_of[first + j] = (first, j, count)

        b1row = work.tile([P, F], BF16, name="b1row", tag="x", bufs=4)
        nc.vector.memset(b1row[:], 0.0)
        ones = const.tile([P, P], BF16, name="ones")
        nc.vector.memset(ones[:], 1.0)
        gbrow = work.tile([P, 2 * D], BF16, name="gbrow", tag="x", bufs=4)
        nc.vector.memset(gbrow[:], 0.0)
        gb = psum.tile([P, 2 * D], BF16, name="gb", tag="gb", bufs=1)

        zs = {}

        def load_z(grp, half=None):
            if half in (None, 0):
                zs[grp] = work.tile([P, GT, D], BF16, name="zs", tag="zs", bufs=4)
            t = zs[grp]
            if half is None:
                nc.sync.dma_start(out=t[:], in_=z_view[:, GT * grp : GT * (grp + 1), :])
            else:
                first = GT * grp + 2 * half
                nc.sync.dma_start(out=t[:, 2 * half : 2 * half + 2, :], in_=z_view[:, first : first + 2, :])

        w1raw = []
        w2raw = []
        w1_view = W1.rearrange("(p j) c -> p j c", j=4)
        for g in range(2):
            t = work.tile([P, 4, 512], BF16, name="w1raw", tag="wr", bufs=4)
            nc.sync.dma_start(out=t[:], in_=w1_view[:, :, 512 * g : 512 * (g + 1)])
            w1raw.append(t)
            load_z(0, g)
            if g == 0:
                nc.sync.dma_start(out=b1row[0:1, :], in_=b1.rearrange("(o f) -> o f", o=1))
        nc.sync.dma_start(out=gbrow[0:1, 0:D], in_=g2.rearrange("(o f) -> o f", o=1))
        nc.sync.dma_start(out=gbrow[0:1, D : 2 * D], in_=be2.rearrange("(o f) -> o f", o=1))
        load_z(1)
        load_z(2)
        for g in range(2):
            t = work.tile([P, 4, 512], BF16, name="w2raw", tag="wr", bufs=4)
            nc.sync.dma_start(out=t[:], in_=W2[512 * g : 512 * (g + 1), :].rearrange("(p j) d -> p j d", j=4))
            w2raw.append(t)
        load_z(3)
        g1b = const.tile([P, 2, 4], BF16, name="g1b")
        nc.sync.dma_start(out=g1b[:], in_=g1.rearrange("(g p t) -> p g t", g=2, t=4))
        be1b = const.tile([P, 2, 4], BF16, name="be1b")
        nc.sync.dma_start(out=be1b[:], in_=be1.rearrange("(g p t) -> p g t", g=2, t=4))
        b2bc = const.tile([P, D], BF16, name="b2bc")

        def load_second_norm():
            nc.sync.dma_start(out=b2bc[:], in_=b2.partition_broadcast(P))

        neg_half = const.tile([P, 8], F32, name="neg_half")
        nc.gpsimd.memset(neg_half[:], -0.5)
        warm = const.tile([P, 1], F32, name="warm")
        nc.scalar.activation(out=warm[:], in_=neg_half[:, 0:1], func=ACT.Gelu)
        ident = const.tile([P, P], F32, name="ident")
        make_identity(nc, ident[:])
        unit = const.tile([P, 8, 2], F32, name="unit")
        nc.gpsimd.memset(unit[:, :, 0:1], -1.0 / F)
        nc.gpsimd.memset(unit[:, :, 1:2], 1.0 / F**3)
        for j in V_STATS:
            nc.gpsimd.memset(unit[:, j, 0:1], -1.0)
            nc.gpsimd.memset(unit[:, j, 1:2], 1.0)
        eps_col = const.tile([P, 1], F32, name="eps_col")
        nc.vector.tensor_scalar(
            out=eps_col[:], in0=neg_half[:, 0:1], scalar1=0.0, scalar2=EPS, op0=ALU.mult, op1=ALU.add
        )

        acts = []
        for i in range(NT):
            acts.append(const.tile([P, F], F32, name="act%d" % i))

        def z_transpose(pr):
            if not 0 <= pr < NPAIR:
                return
            grp, h = divmod(pr, 2)
            zt = psum.tile([P, 2, 2, P], F32, name="zt", tag="pb", bufs=3)
            for jj in range(2):
                words = zs[grp][:, 2 * h + jj, :].bitcast(F32)
                for u in range(2):
                    nc.tensor.transpose(zt[:, jj, u, :], words[:, u:256:2], ident[:])
            live["zt", pr] = zt

        def z_copy(pr):
            if not 0 <= pr < NPAIR:
                return
            grp, h = divmod(pr, 2)
            if h == 0:
                live["zg", grp] = work.tile([P, GT * P * 4], BF16, name="zg", tag="zg", bufs=4, align_bytes=64)
            zgw = live["zg", grp][:].bitcast(F32).rearrange("p (j r u) -> p j r u", j=GT, u=2)
            if pr >= V_ZCOPY:
                nc.vector.tensor_copy(out=zgw[:, 2 * h : 2 * h + 2, :, :], in_=live["zt", pr][:].rearrange("p j u r -> p j r u"))
            else:
                nc.scalar.copy(out=zgw[:, 2 * h : 2 * h + 2, :, :], in_=live["zt", pr][:].rearrange("p j u r -> p j r u"))

        def z_quantise(grp, half=None):
            if not ok(grp):
                return
            if half in (None, 0):
                zc = work.tile([P, GT * P], U32, name="zc", tag="codes", bufs=4, align_bytes=64)
                zsc = work.tile([P, GT * P], U8, name="zsc", tag="scales", bufs=4, align_bytes=64)
                live["zq", grp] = (zc, zsc)
            zc, zsc = live["zq", grp]
            if half is None:
                nc.vector.quantize_mx(out=zc[:].bitcast(FP8X4), scales=zsc[:], in_=live["zg", grp][:])
            else:
                c = slice(2 * P * half, 2 * P * (half + 1))
                nc.vector.quantize_mx(
                    out=zc[:, c].bitcast(FP8X4), scales=zsc[:, c], in_=live["zg", grp][:, 8 * P * half : 8 * P * (half + 1)]
                )

        def matmul_1(i):
            if not tile_ok(i):
                return
            zc, zsc = live["zq", i // GT]
            cols = slice(P * (i % GT), P * (i % GT + 1))
            u = psum.tile([P, F], BF16, name="u", tag="pa", bufs=4)
            nc.tensor.matmul_mx(
                out=u[:],
                lhsT=zc[:, cols].bitcast(FP8X4),
                lhsT_scale=zsc[:, cols],
                rhs=w1c[:].bitcast(FP8X4),
                rhs_scale=w1s[:],
                start=True,
                stop=True,
            )
            live["u", i] = u

        def add_b1(i):
            if not tile_ok(i):
                return
            x = work.tile([P, F], F32, name="x", tag="x", bufs=4)
            nc.vector.tensor_tensor(out=x[:], in0=live["u", i][:], in1=b1p[:], op=ALU.add)
            live["x", i] = x

        def gelu(i):
            if not tile_ok(i):
                return
            first, j, count = batch_of[i]
            if j == 0:
                live["raw", first] = stats.tile([P, 8, 2], F32, name="raw", tag="raw")
            if i % 8 not in V_STATS or i >= LATE:
                nc.scalar.activation(
                    out=acts[i][:], in_=live["x", i][:], func=ACT.Gelu, accum_out=live["raw", first][:, j, 0:1]
                )
            else:
                nc.scalar.activation(out=acts[i][:], in_=live["x", i][:], func=ACT.Gelu)

        def stats_1(i):
            if not tile_ok(i):
                return
            first, j, count = batch_of[i]
            raw = live["raw", first]
            if i % 8 not in V_STATS or i >= LATE:
                junk = work.tile([P, F], BF16, name="junk", tag="junk", bufs=2)
                nc.scalar.activation(
                    out=junk[:],
                    in_=acts[i][:],
                    func=ACT.Square,
                    scale=-float(F),
                    bias=raw[:, j, 0:1],
                    accum_out=raw[:, j, 1:2],
                )
            else:
                bs = stats.tile([P, 2, 6], F32, name="bs", tag="bs")
                for c in range(2):
                    nc.vector.bn_stats(out=bs[:, c, :], in_=acts[i][:, 512 * c : 512 * (c + 1)])
                live["bs", i] = bs

        def aggregate_1(i):
            if not tile_ok(i) or i % 8 not in V_STATS or i >= LATE:
                return
            first, j, count = batch_of[i]
            nc.vector.bn_aggr(out=live["raw", first][:, j, :], in_=live["bs", i][:].rearrange("p c s -> p (c s)"))

        def rstd_1(first, count):
            mv = stats.tile([P, 8, 2], F32, name="mv", tag="mv")
            nc.gpsimd.tensor_tensor(
                out=mv[:, 0:count, :], in0=live["raw", first][:, 0:count, :], in1=unit[:, first % 8 : first % 8 + count, :], op=ALU.mult
            )
            ve = stats.tile([P, 8], F32, name="ve", tag="ve")
            nc.gpsimd.tensor_scalar(
                out=ve[:, 0:count], in0=mv[:, 0:count, 1], scalar1=1.0, scalar2=EPS, op0=ALU.mult, op1=ALU.add
            )
            rs = stats.tile([P, 8], F32, name="rs", tag="rs")
            nc.gpsimd.tensor_tensor(out=rs[:, 0:count], in0=ve[:, 0:count], in1=neg_half[:, 0:count], op=ALU.pow)
            live["mv", first] = mv
            live["rs", first] = rs

        def rstd_late(grp):
            raw = live["raw", LATE]
            nm = stats.tile([P, 4], F32, name="nm", tag="nm")
            nc.gpsimd.tensor_scalar(
                out=nm[:], in0=raw[:, 0:4, 0], scalar1=live["go2", grp][:, 0:1], scalar2=-1.0 / F, op0=ALU.mult, op1=ALU.mult
            )
            ve = stats.tile([P, 8], F32, name="ve", tag="ve")
            nc.gpsimd.tensor_scalar(
                out=ve[:, 0:4], in0=raw[:, 0:4, 1], scalar1=1.0 / F**3, scalar2=EPS, op0=ALU.mult, op1=ALU.add
            )
            rs = stats.tile([P, 8], F32, name="rs", tag="rs")
            nc.gpsimd.tensor_tensor(out=rs[:, 0:4], in0=ve[:, 0:4], in1=neg_half[:, 0:4], op=ALU.pow)
            nr = stats.tile([P, 4], F32, name="nr", tag="nr")
            nc.gpsimd.tensor_tensor(out=nr[:], in0=nm[:], in1=rs[:, 0:4], op=ALU.mult)
            live["rs", LATE] = rs
            live["nr", LATE] = nr

        def normalise_late(i):
            j = i - LATE
            nc.scalar.activation(
                out=acts[i][:],
                in_=acts[i][:],
                func=ACT.Identity,
                scale=live["rs", LATE][:, j : j + 1],
                bias=live["nr", LATE][:, j : j + 1],
            )

        def normalise(i):
            first, j, count = batch_of[i]
            nc.gpsimd.tensor_scalar(
                out=acts[i][:],
                in0=acts[i][:],
                scalar1=live["mv", first][:, j, 0:1],
                scalar2=live["rs", first][:, j : j + 1],
                op0=ALU.add,
                op1=ALU.mult,
            )

        def h_transpose(n, warm=False):
            grp, blk = divmod(n, 8)
            if not okh(grp):
                return
            ht = psum.tile([P, SIZES[grp] * P], F32, name="ht", tag="pa", bufs=4)
            if warm:
                nc.tensor.matmul(out=ht[:], lhsT=ones[:], rhs=b1p[:, 0:512], start=True, stop=True)
            for i in range(SIZES[grp]):
                nc.tensor.transpose(
                    ht[:, P * i : P * (i + 1)], acts[STARTS[grp] + i][:, P * blk : P * (blk + 1)], ident[:]
                )
            live["ht", grp, blk] = ht

        def affine_1(grp, blk):
            if not okh(grp):
                return
            q, t = divmod(blk, 4)
            if ("hT", grp, q) not in live:
                live["hT", grp, q] = work.tile([P, 4, SIZES[grp] * P], BF16, name="hT", tag="wr", bufs=4)
            if 8 * grp + blk in V_BANKS:
                nc.vector.tensor_scalar(
                    out=live["hT", grp, q][:, t, :],
                    in0=live["ht", grp, blk][:],
                    scalar1=g1c[:, blk : blk + 1],
                    scalar2=be1c[:, blk : blk + 1],
                    op0=ALU.mult,
                    op1=ALU.add,
                )
            else:
                nc.scalar.activation(
                    out=live["hT", grp, q][:, t, :],
                    in_=live["ht", grp, blk][:],
                    func=ACT.Identity,
                    scale=g1c[:, blk : blk + 1],
                    bias=be1c[:, blk : blk + 1],
                )

        def interleave(grp, q):
            if not okh(grp):
                return
            hg = work.tile([P, SIZES[grp] * P, 4], BF16, name="hg", tag="wg", bufs=3, align_bytes=64)
            dst = hg[:].rearrange("p (c i) t -> p c t i", i=4)
            src = live["hT", grp, q][:].rearrange("p t (c i) -> p c t i", i=4)
            if grp <= 0:
                nc.vector.tensor_copy(out=dst, in_=src)
            elif (grp, q) == S_INTERLEAVE:
                nc.scalar.copy(out=hg[:], in_=live["hT", grp, q][:].rearrange("p t n -> p n t"))
            else:
                nc.gpsimd.tensor_scalar(
                    out=hg[:],
                    in0=live["hT", grp, q][:].rearrange("p t n -> p n t"),
                    scalar1=live["go2", grp][:, 0:1],
                    scalar2=0.0,
                    op0=ALU.mult,
                    op1=ALU.add,
                )
            live["hg", grp, q] = hg

        def let_go2(grp):
            if not okh(grp):
                return
            go2 = stats.tile([P, 1], F32, name="go2", tag="go2")
            nc.vector.tensor_scalar(
                out=go2[:], in0=neg_half[:, 0:1], scalar1=0.0, scalar2=1.0, op0=ALU.mult, op1=ALU.add
            )
            live["go2", grp] = go2

        def h_quantise(grp, q):
            if not okh(grp):
                return
            hc = work.tile([P, SIZES[grp] * P], U32, name="hc", tag="codes", bufs=4, align_bytes=64)
            hs = work.tile([P, SIZES[grp] * P], U8, name="hs", tag="scales", bufs=4, align_bytes=64)
            nc.vector.quantize_mx(
                out=hc[:].bitcast(FP8X4), scales=hs[:], in_=live["hg", grp, q][:].rearrange("p n t -> p (n t)")
            )
            live["hq", grp, q] = (hc, hs)

        def matmul_2(grp, i):
            if not okh(grp):
                return
            cols = slice(P * i, P * (i + 1))
            o = psum.tile([P, D], F32, name="o", tag="pb", bufs=3)
            for q in range(2):
                hc, hs = live["hq", grp, q]
                nc.tensor.matmul_mx(
                    out=o[:],
                    lhsT=hc[:, cols].bitcast(FP8X4),
                    lhsT_scale=hs[:, cols],
                    rhs=w2c[q][:].bitcast(FP8X4),
                    rhs_scale=w2s[q][:],
                    start=(q == 0),
                    stop=(q == 1),
                )
            live["o", grp, i] = o

        def add_b2(grp, i):
            if not okh(grp):
                return
            if i == 0:
                live["sy", grp] = stats.tile([P, GT], F32, name="sy", tag="sy")
            if i % 2 == 0:
                live["y", grp, i // 2] = work.tile([P, 2, D], F32, name="y", tag="zs", bufs=4)
            nc.vector.scalar_tensor_tensor(
                out=live["y", grp, i // 2][:, i % 2, :],
                in0=live["o", grp, i][:],
                scalar=1.0,
                in1=b2bc[:],
                op0=ALU.mult,
                op1=ALU.add,
                accum_out=live["sy", grp][:, i : i + 1],
            )

        def square_2(grp, i):
            if not okh(grp):
                return
            if i == 0:
                live["sq2", grp] = stats.tile([P, GT], F32, name="sq2", tag="sq2")
            junk2 = work.tile([P, D], BF16, name="junk2", tag="junk", bufs=2)
            nc.scalar.activation(
                out=junk2[:],
                in_=live["y", grp, i // 2][:, i % 2, :],
                func=ACT.Square,
                scale=-float(D),
                bias=live["sy", grp][:, i : i + 1],
                accum_out=live["sq2", grp][:, i : i + 1],
            )

        def neg_mean_2(grp):
            if not okh(grp):
                return
            nm2 = stats.tile([P, GT], F32, name="nm2", tag="nm2")
            n = SIZES[grp]
            nc.vector.tensor_scalar(
                out=nm2[:, 0:n], in0=live["sy", grp][:, 0:n], scalar1=-1.0 / D, scalar2=None, op0=ALU.mult
            )
            live["nm2", grp] = nm2

        def rstd_2(grp, first=0, n=GT):
            if not okh(grp):
                return
            if ("rs2", grp) not in live:
                live["rs2", grp] = stats.tile([P, GT], F32, name="rs2", tag="rs2")
            nc.scalar.activation(
                out=live["rs2", grp][:, first:n],
                in_=live["sq2", grp][:, first:n],
                func=ACT.Abs_reciprocal_sqrt,
                scale=1.0 / D**3,
                bias=eps_col[:, 0:1],
            )

        def centre_gain(grp, i):
            if not okh(grp):
                return
            if i % 2 == 0:
                live["q", grp, i // 2] = work.tile([P, 2, D], F32, name="q", tag="x", bufs=4)
            nc.vector.scalar_tensor_tensor(
                out=live["q", grp, i // 2][:, i % 2, :],
                in0=live["y", grp, i // 2][:, i % 2, :],
                scalar=live["nm2", grp][:, i : i + 1],
                in1=gb[:, 0:D],
                op0=ALU.add,
                op1=ALU.mult,
            )

        def scale_shift(grp, i):
            if not okh(grp):
                return
            if i % 2 == 0:
                live["ot", grp, i // 2] = work.tile([P, 2, D], F32, name="ot", tag="zg", bufs=4, align_bytes=64)
            nc.vector.scalar_tensor_tensor(
                out=live["ot", grp, i // 2][:, i % 2, :],
                in0=live["q", grp, i // 2][:, i % 2, :],
                scalar=live["rs2", grp][:, i : i + 1],
                in1=gb[:, D : 2 * D],
                op0=ALU.mult,
                op1=ALU.add,
            )

        def finish_on_gpsimd(grp, i):
            if i % 2 == 0:
                live["q", grp, i // 2] = work.tile([P, 2, D], F32, name="q", tag="x", bufs=4)
                live["ot", grp, i // 2] = work.tile([P, 2, D], F32, name="ot", tag="wr", bufs=4)
            q = live["q", grp, i // 2][:, i % 2, :]
            if ("nr2", grp) not in live:
                live["nr2", grp] = stats.tile([P, GT], F32, name="nr2", tag="nr2")
            nc.scalar.activation(
                out=live["nr2", grp][:, i : i + 1],
                in_=live["nm2", grp][:, i : i + 1],
                func=ACT.Identity,
                scale=live["rs2", grp][:, i : i + 1],
            )
            nc.scalar.activation(
                out=q,
                in_=live["y", grp, i // 2][:, i % 2, :],
                func=ACT.Identity,
                scale=live["rs2", grp][:, i : i + 1],
                bias=live["nr2", grp][:, i : i + 1],
            )
            nc.gpsimd.tensor_tensor(out=q, in0=q, in1=gbs[:, 0:D], op=ALU.mult)
            nc.gpsimd.tensor_tensor(out=live["ot", grp, i // 2][:, i % 2, :], in0=q, in1=gbs[:, D : 2 * D], op=ALU.add)

        def store(grp, half):
            if not okh(grp):
                return
            first = STARTS[grp] + 2 * half
            nc.sync.dma_start(out=out_view[:, first : first + 2, :], in_=live["ot", grp, half][:])

        def store_one(grp, i):
            nc.sync.dma_start(out=out_view[:, STARTS[grp] + i, :], in_=live["ot", grp, i // 2][:, i % 2, :])

        z_transpose(0)
        w1g = []
        for g in range(2):
            w1g.append(work.tile([P, 2048], BF16, name="w1g", tag="wg", bufs=3, align_bytes=64))
        dst = [w1g[g][:].rearrange("p (t m j) -> p t m j", t=4, j=4) for g in range(2)]
        src = [w1raw[g][:].rearrange("p j (m t) -> p t m j", t=4) for g in range(2)]
        w1c = const.tile([P, F], U32, name="w1c", align_bytes=64)
        w1s = const.tile([P, F], U8, name="w1s", align_bytes=64)
        nc.vector.tensor_copy(out=dst[0][:, 0:2], in_=src[0][:, 0:2])
        nc.vector.tensor_copy(out=dst[0][:, 2:4], in_=src[0][:, 2:4])
        z_copy(0)
        nc.vector.quantize_mx(out=w1c[:, 0:512].bitcast(FP8X4), scales=w1s[:, 0:512], in_=w1g[0][:])
        b1ps = []
        for g in range(2):
            b1ps.append(psum.tile([P, 512], F32, name="b1ps", tag="pa", bufs=4))
            nc.tensor.matmul(out=b1ps[g][:], lhsT=ones[:], rhs=b1row[:, 512 * g : 512 * (g + 1)], start=True, stop=True)
        z_transpose(1)
        nc.vector.tensor_copy(out=dst[1][:, 0:2], in_=src[1][:, 0:2])
        nc.scalar.copy(out=dst[1][:, 2:4], in_=src[1][:, 2:4])
        z_quantise(0, 0)
        b1p = const.tile([P, F], BF16, name="b1p")
        for g in range(2):
            nc.scalar.copy(
                out=b1p[:, 512 * g : 512 * (g + 1)].rearrange("p (t m) -> p t m", t=4),
                in_=b1ps[g][:].rearrange("p (m t) -> p t m", t=4),
            )
        z_copy(1)
        nc.vector.quantize_mx(out=w1c[:, 512:1024].bitcast(FP8X4), scales=w1s[:, 512:1024], in_=w1g[1][:])
        go = [const.tile([P, 1], F32, name="go%d" % g) for g in range(2)]

        def let_go(g):
            nc.vector.tensor_scalar(
                out=go[g][:], in0=neg_half[:, 0:1], scalar1=0.0, scalar2=1.0, op0=ALU.mult, op1=ALU.add
            )

        g1c = const.tile([P, 8], F32, name="g1c")
        be1c = const.tile([P, 8], F32, name="be1c")
        matmul_1(0)

        w2g = []
        w2c, w2s = [], []

        def group_w2(g):
            w2g.append(work.tile([P, 512, 4], BF16, name="w2g", tag="wg", bufs=3, align_bytes=64))
            nc.gpsimd.tensor_scalar(
                out=w2g[g][:],
                in0=w2raw[g][:].rearrange("p j d -> p d j"),
                scalar1=go[g][:, 0:1],
                scalar2=0.0,
                op0=ALU.mult,
                op1=ALU.add,
            )


        def quantise_w2():
            for g in range(2):
                w2c.append(const.tile([P, 512], U32, name="w2c%d" % g, align_bytes=64))
                w2s.append(const.tile([P, 512], U8, name="w2s%d" % g, align_bytes=64))
                nc.vector.quantize_mx(
                    out=w2c[g][:].bitcast(FP8X4), scales=w2s[g][:], in_=w2g[g][:].rearrange("p d j -> p (d j)")
                )

        late_loads = {0: [4, 5], 4: [6], 8: [7]}
        batch_end = {}
        for first, count in BATCHES:
            batch_end[first + count - 1] = (first, count)
        for t in range(NT + 1):
            for grp in late_loads.get(t, []):
                load_z(grp)
            matmul_1(t + 1)
            for pr in range(2, NPAIR):
                if max(2 * pr - 8, pr - 2) == t:
                    z_transpose(pr)
            add_b1(t)
            if t == 0:
                z_quantise(0, 1)
                let_go(0)
                group_w2(0)
            aggregate_1(t - 3)
            for pr in range(2, NPAIR):
                if max(2 * pr - 6, pr - 1) == t:
                    z_copy(pr)
            gelu(t - 1)
            if t - 2 < LATE:
                stats_1(t - 2)
            if t == 2:
                z_quantise(1)
            if t % 4 == 1 and t > 1:
                z_quantise((t + 3) // 4)
            if t == 2:
                let_go(1)
                group_w2(1)
                nc.gpsimd.tensor_copy(out=g1c[:], in_=g1b[:].rearrange("p g t -> p (g t)"))
                nc.gpsimd.tensor_copy(out=be1c[:], in_=be1b[:].rearrange("p g t -> p (g t)"))
            if t == 1:
                for g in range(2):
                    nc.tensor.matmul(
                        out=gb[:, D * g : D * (g + 1)], lhsT=ones[:], rhs=gbrow[:, D * g : D * (g + 1)], start=True, stop=True
                    )
            if t == 12:
                load_second_norm()
            if t == 4:
                quantise_w2()
            if t == NT:
                for n in range(4):
                    h_transpose(n)
            if t - 2 in batch_end and t - 2 < LATE:
                first, count = batch_end[t - 2]
                rstd_1(first, count)
                for j in range(count):
                    normalise(first + j)

        def evac(b):
            affine_1(b // 8, b % 8)

        def tile_of(n):
            return divmod(n, 4) if 0 <= n < NT else (-1, 0)

        gbs = const.tile([P, 2 * D], BF16, name="gbs")
        for b in range(4):
            evac(b)
            h_transpose(b + 4)
        interleave(0, 0)
        for b in range(4, 8):
            evac(b)
            h_transpose(b + 4)
        interleave(0, 1)
        for b in range(8, 12):
            evac(b)
            if b < 10:
                h_transpose(b + 4)
        for tau in range(NT + 9):
            g, i = divmod(tau, 4)
            if i == 0:
                add_b2(*tile_of(tau - 1))
                h_quantise(g, 0)
                neg_mean_2(g - 1)
                h_quantise(g, 1)
                let_go2(g + 1)
            h_transpose(2 * tau + 14, WARM)
            h_transpose(2 * tau + 15)
            if tau < NT:
                matmul_2(g, i)
            if i == 0:
                interleave(g + 1, 0)
            if i == 2 and (g + 1, 1) != S_INTERLEAVE:
                interleave(g + 1, 1)
            evac(2 * tau + 12)
            if i == 2 and g < NH:
                rstd_2(g - 1, 2 if g - 1 == EARLY_RSTD else 0)
            if i == 0 and g - 1 == EARLY_RSTD:
                rstd_2(g - 1, 0, 2)
            if tau == NT + 1:
                square_2(*tile_of(NT - 1))
                rstd_2(NH - 1)
            evac(2 * tau + 13)
            if tau == 8:
                nc.scalar.copy(out=gbs[:], in_=gb[:])
            for n in range(NT):
                if n + (LAG if n < NT - 4 else LAG_END) == tau and n not in G_TILES:
                    scale_shift(*tile_of(n))
                    if n >= ONE_BY_ONE:
                        store_one(*tile_of(n))
                    elif n % 2 == 1:
                        store(n // 4, (n % 4) // 2)
            if tau - 4 not in G_TILES:
                centre_gain(*tile_of(tau - 4))
            for n in G_TILES:
                if G_TILES[n][0] == tau:
                    finish_on_gpsimd(*tile_of(n))
                    if n == 22:
                        interleave(*S_INTERLEAVE)
                if G_TILES[n][1] == tau:
                    store_one(*tile_of(n))
            if i != 0:
                add_b2(*tile_of(tau - 1))
            if tau != NT + 1:
                square_2(*tile_of(tau - 2))
            for n in LATE_SQUARES.get(tau, []):
                stats_1(n)
            if tau == 3:
                rstd_late(1)
            if tau in LATE_NORMALISE:
                normalise_late(LATE_NORMALISE[tau])
